import numpy as np
import ml_dtypes


def mxq(x, axis, fmt="e4m3"):
    dtype, down = {"e4m3": (ml_dtypes.float8_e4m3fn, 7), "e5m2": (ml_dtypes.float8_e5m2, 14)}[fmt]
    v = np.moveaxis(np.asarray(x, np.float32).astype(ml_dtypes.bfloat16).astype(np.float64), axis, -1)
    blocks = v.reshape(v.shape[:-1] + (-1, 32))
    amax = np.abs(blocks).max(-1, keepdims=True)
    byte = np.maximum(np.where(amax > 0, np.frexp(amax)[1] - 1 + 127, 0) - down, 1)
    scale = np.exp2(byte - 127.0)
    codes = (blocks / scale).astype(np.float32).astype(dtype).astype(np.float64)
    return np.moveaxis((codes * scale).reshape(v.shape), -1, axis)


WIDE = False


def mx_kscale(k):
    if not WIDE:
        return np.ones(k)
    levels = np.array([10, -10, 5, -5, 0])
    a = np.random.permutation(np.resize(levels, k // 512 * 4)).reshape(k // 512, 4)
    idx = np.arange(k)
    return np.exp2(a[idx // 512, idx % 128 // 32])


BF16 = ml_dtypes.bfloat16


def bf(x):
    return np.asarray(x, np.float32).astype(BF16)


def f64(x):
    return np.asarray(x).astype(np.float64)


B, K, N = 1024, 1024, 1024


def setup_inputs():
    s = mx_kscale(K)
    s = s / s.max()
    return {"x": bf(np.random.standard_normal((B, K)) * s),
            "W": bf(np.random.standard_normal((K, N)) * 0.4 / np.sqrt(K) / s[:, None]),
            "P": bf(np.random.standard_normal(N) * 0.3),
            "w": bf(0.8 + 0.1 * np.random.standard_normal(1)),
            "p": bf(0.5 + 0.1 * np.random.standard_normal(1)),
            "sine_w": bf(1.2 + 0.1 * np.random.standard_normal(1)),
            "cosine_w": bf(-0.7 + 0.1 * np.random.standard_normal(1))}


def reference(x, W, P, w, p, sine_w, cosine_w):
    x = f64(x)
    original = f64(w) * x + f64(p)
    z = (mxq(x, 1, "e4m3") @ mxq(f64(W), 0, "e4m3")) + f64(P)
    periodic = f64(sine_w) * np.sin(z) + f64(cosine_w) * np.cos(z)
    return np.concatenate((original, periodic), axis=-1)

@@ -1,0 +1,256 @@
+import math
+from contextlib import ExitStack
+
+import concourse.mybir as mybir
+from concourse.masks import make_identity
+
+F32 = mybir.dt.float32
+BF16 = mybir.dt.bfloat16
+U32 = mybir.dt.uint32
+U8 = mybir.dt.uint8
+FP8X4 = mybir.dt.float8_e4m3fn_x4
+ALU = mybir.AluOpType
+ACT = mybir.ActivationFunctionType
+
+FLOPS = 2 * 1024 * 1024 * 1024
+
+NP = 128
+B = 1024
+K = 1024
+N = 1024
+NT = B // NP
+NG = K // 512
+NH = N // 512
+TURN = 1.0 / (2.0 * math.pi)
+MAGIC = 12582912.0
+GUARD = 1e-30
+PI_BELOW = 3.1415925025939941
+
+
+def tile_time2vec_kernel(tc, x, W, P, w, p, sine_w, cosine_w, out):
+    nc = tc.nc
+    with ExitStack() as ctx:
+        keep = ctx.enter_context(tc.tile_pool(name="keep", bufs=1))
+        small = ctx.enter_context(tc.tile_pool(name="small", bufs=1))
+        linp = ctx.enter_context(tc.tile_pool(name="linp", bufs=4))
+        epi = ctx.enter_context(tc.tile_pool(name="epi", bufs=3))
+        psum = ctx.enter_context(tc.psum_pool(name="psum", bufs=8))
+
+        x_view = x.rearrange("(p t) k -> p t k", t=NT)
+        out_view = out.rearrange("(p t) n -> p t n", t=NT)
+        w_view = W.rearrange("(g u q e) c -> g q u (e c)", g=NG, u=2, q=NP, e=2)
+
+        warm = small.tile([NP, 1], F32)
+        nc.vector.memset(warm[:], 0.0)
+        junk = small.tile([NP, 1], F32)
+        nc.scalar.activation(out=junk[:], in_=warm[:], func=ACT.Sin)
+        ones = keep.tile([NP, NP], BF16)
+        nc.vector.memset(ones[:], 1.0)
+        prow = keep.tile([NP, N], BF16)
+        nc.vector.memset(prow[:], 0.0)
+        ident = keep.tile([NP, NP], F32)
+        make_identity(nc, ident[:])
+
+        raw16 = small.tile([NP, 4, 16], BF16)
+        with nc.allow_non_contiguous_dma(reason="four scalars, one element a partition"):
+            for j, src in enumerate((w, p, cosine_w, sine_w)):
+                nc.scalar.dma_start(out=raw16[:, j, 0:1], in_=src.partition_broadcast(NP))
+        nc.scalar.dma_start(out=prow[0:1, :], in_=P.rearrange("(o n) -> o n", o=1))
+
+        x_sb = keep.tile([NP, NT, K], BF16)
+        w_raw = keep.tile([NP, NG, 4, N], BF16)
+
+        def load_x(j):
+            nc.sync.dma_start(out=x_sb[:, 2 * j : 2 * j + 2, :], in_=x_view[:, 2 * j : 2 * j + 2, :])
+
+        def load_w(g):
+            nc.sync.dma_start(
+                out=w_raw[:, g].rearrange("p (u e) c -> p u (e c)", u=2), in_=w_view[g]
+            )
+
+        load_x(0)
+        load_w(0)
+        load_x(1)
+        load_w(1)
+        load_x(2)
+        load_x(3)
+
+        pbs = []
+        for h in range(NH):
+            pb = psum.tile([NP, 512], F32, tag="bank", name="pb%d" % h)
+            nc.tensor.matmul(out=pb[:], lhsT=ones[:], rhs=prow[:, 512 * h : 512 * h + 512], start=True, stop=True)
+            pbs.append(pb)
+
+        def col(name):
+            return small.tile([NP, 1], F32, name=name)
+
+        sc32 = small.tile([NP, 4], F32)
+        nc.vector.tensor_scalar(out=sc32[:], in0=raw16[:, :, 0], scalar1=GUARD, scalar2=None, op0=ALU.add)
+        w32 = sc32[:, 0:1]
+        p32 = sc32[:, 1:2]
+        sg2 = col("sg2")
+        nc.vector.tensor_scalar(out=sg2[:], in0=sc32[:, 3:4], scalar1=0.0, scalar2=2.0, op0=ALU.is_ge, op1=ALU.mult)
+        cs1 = small.tile([NP, 2], F32)
+        nc.vector.scalar_tensor_tensor(
+            out=cs1[:], in0=sc32[:, 2:4], scalar=sg2[:], in1=sc32[:, 2:4], op0=ALU.mult, op1=ALU.subtract
+        )
+        c1 = cs1[:, 0:1]
+        s1 = cs1[:, 1:2]
+        absc = col("absc")
+        nc.vector.scalar_tensor_tensor(out=absc[:], in0=c1, scalar=-1.0, in1=c1, op0=ALU.mult, op1=ALU.max)
+        den = col("den")
+        nc.vector.tensor_scalar(out=den[:], in0=absc[:], scalar1=s1, scalar2=None, op0=ALU.add)
+        rden = col("rden")
+        nc.vector.reciprocal(out=rden[:], in_=den[:])
+        ang = small.tile([NP, 2], F32)
+        nc.vector.tensor_scalar(
+            out=ang[:, 0:1], in0=c1, scalar1=rden[:], scalar2=0.5 * math.pi, op0=ALU.mult, op1=ALU.mult
+        )
+        nc.vector.tensor_scalar(
+            out=ang[:, 1:2], in0=ang[:, 0:1], scalar1=0.5 * math.pi, scalar2=PI_BELOW, op0=ALU.add, op1=ALU.min
+        )
+        sico = small.tile([NP, 2], F32)
+        nc.scalar.activation(out=sico[:], in_=ang[:], func=ACT.Sin)
+        tsin = small.tile([NP, 2], F32)
+        nc.vector.tensor_scalar(out=tsin[:], in0=cs1[:], scalar1=sico[:, 0:1], scalar2=None, op0=ALU.mult)
+        dd = col("dd")
+        nc.vector.scalar_tensor_tensor(
+            out=dd[:], in0=s1, scalar=sico[:, 1:2], in1=tsin[:, 0:1], op0=ALU.mult, op1=ALU.add
+        )
+        nn = col("nn")
+        nc.vector.scalar_tensor_tensor(
+            out=nn[:], in0=c1, scalar=sico[:, 1:2], in1=tsin[:, 1:2], op0=ALU.mult, op1=ALU.subtract
+        )
+        rdd = col("rdd")
+        nc.vector.reciprocal(out=rdd[:], in_=dd[:])
+        tau = col("tau")
+        nc.vector.tensor_scalar(out=tau[:], in0=nn[:], scalar1=rdd[:], scalar2=None, op0=ALU.mult)
+        tau2 = col("tau2")
+        nc.vector.tensor_scalar(out=tau2[:], in0=tau[:], scalar1=tau[:], scalar2=None, op0=ALU.mult)
+        tauc = col("tauc")
+        nc.vector.tensor_scalar(out=tauc[:], in0=tau[:], scalar1=TURN, scalar2=None, op0=ALU.mult)
+        phi0c = col("phi0c")
+        nc.vector.tensor_scalar(out=phi0c[:], in0=ang[:, 0:1], scalar1=TURN, scalar2=None, op0=ALU.mult)
+        h1 = col("h1")
+        nc.vector.tensor_scalar(out=h1[:], in0=tau2[:], scalar1=-1.0 / 7.0, scalar2=0.2, op0=ALU.mult, op1=ALU.add)
+        h2 = col("h2")
+        nc.vector.tensor_scalar(out=h2[:], in0=h1[:], scalar1=tau2[:], scalar2=-1.0 / 3.0, op0=ALU.mult, op1=ALU.add)
+        h3 = col("h3")
+        nc.vector.tensor_scalar(out=h3[:], in0=h2[:], scalar1=tau2[:], scalar2=1.0, op0=ALU.mult, op1=ALU.add)
+        phit = col("phit")
+        nc.vector.tensor_scalar(out=phit[:], in0=h3[:], scalar1=tauc[:], scalar2=phi0c[:], op0=ALU.mult, op1=ALU.add)
+        g1 = col("g1")
+        nc.vector.tensor_scalar(out=g1[:], in0=tau2[:], scalar1=1.0 / 16.0, scalar2=-0.125, op0=ALU.mult, op1=ALU.add)
+        g2 = col("g2")
+        nc.vector.tensor_scalar(out=g2[:], in0=g1[:], scalar1=tau2[:], scalar2=0.5, op0=ALU.mult, op1=ALU.add)
+        g3 = col("g3")
+        nc.vector.tensor_scalar(out=g3[:], in0=g2[:], scalar1=tau2[:], scalar2=1.0, op0=ALU.mult, op1=ALU.add)
+        dsg = col("dsg")
+        nc.vector.scalar_tensor_tensor(out=dsg[:], in0=dd[:], scalar=sg2[:], in1=dd[:], op0=ALU.mult, op1=ALU.subtract)
+        amp = col("amp")
+        nc.vector.tensor_scalar(out=amp[:], in0=g3[:], scalar1=dsg[:], scalar2=None, op0=ALU.mult)
+
+        b_sb = keep.tile([NP, N], F32)
+        for h in range(NH):
+            nc.scalar.activation(
+                out=b_sb[:, 512 * h : 512 * h + 512], in_=pbs[h][:], func=ACT.Identity, scale=TURN, bias=phit[:]
+            )
+
+        xg = keep.tile([NP, NT, K], BF16, align_bytes=64)
+        xc = keep.tile([NP, NT, NG, NP], U32, align_bytes=64)
+        xs = keep.tile([NP, NT, NG, NP], U8, align_bytes=64)
+        wg = keep.tile([NP, NG, N, 4], BF16, align_bytes=64)
+        wc = keep.tile([NP, NG, N], U32, align_bytes=64)
+        ws = keep.tile([NP, NG, N], U8, align_bytes=64)
+
+        def x_tile(t):
+            xt = psum.tile([NP, 4, NP], F32, tag="bank", name="xt%d" % t)
+            xw = x_sb[:, t, :].bitcast(F32)
+            for j in range(4):
+                nc.tensor.transpose(out=xt[:, j, :], in_=xw[:, NP * j : NP * j + NP], identity=ident[:])
+            nc.scalar.copy(
+                out=xg[:, t, :].bitcast(F32).rearrange("p (g b u) -> p g b u", g=NG, b=NP, u=2),
+                in_=xt[:].rearrange("p (g u) b -> p g b u", g=NG, u=2),
+            )
+
+        def x_quant(t):
+            nc.vector.quantize_mx(
+                out=xc[:, t].rearrange("p g b -> p (g b)").bitcast(FP8X4),
+                scales=xs[:, t].rearrange("p g b -> p (g b)"),
+                in_=xg[:, t, :],
+            )
+
+        def linear(t):
+            lin = linp.tile([NP, K], F32, name="lin")
+            nc.scalar.activation(out=lin[:], in_=x_sb[:, t, :], func=ACT.Identity, scale=w32, bias=p32)
+            nc.sync.dma_start(out=out_view[:, t, 0:K], in_=lin[:])
+
+        def w_regroup(g, h):
+            cols = slice(512 * h, 512 * h + 512)
+            nc.vector.tensor_copy(
+                out=wg[:, g, cols, :].rearrange("p (c i) t -> p c t i", i=4),
+                in_=w_raw[:, g, :, cols].rearrange("p t (c i) -> p c t i", i=4),
+            )
+
+        def w_quant(g, h):
+            cols = slice(512 * h, 512 * h + 512)
+            nc.vector.quantize_mx(
+                out=wc[:, g, cols].bitcast(FP8X4),
+                scales=ws[:, g, cols],
+                in_=wg[:, g, cols, :].rearrange("p c t -> p (c t)"),
+            )
+
+        x_tile(0)
+        x_tile(1)
+        w_regroup(0, 0)
+        w_regroup(0, 1)
+        x_quant(0)
+        w_quant(0, 0)
+        x_quant(1)
+        w_quant(0, 1)
+        linear(0)
+        linear(1)
+        x_tile(2)
+        x_tile(3)
+        w_regroup(1, 0)
+        w_regroup(1, 1)
+        x_quant(2)
+        w_quant(1, 0)
+        x_quant(3)
+        w_quant(1, 1)
+        linear(2)
+        linear(3)
+        for t in range(4, NT):
+            x_tile(t)
+        for t in range(4, NT):
+            x_quant(t)
+        for t in range(4, NT):
+            linear(t)
+
+        for t in range(NT):
+            v = epi.tile([NP, N], F32, name="v")
+            for h in range(NH):
+                cols = slice(512 * h, 512 * h + 512)
+                z = psum.tile([NP, 512], F32, tag="bank", name="z")
+                for g in range(NG):
+                    nc.tensor.matmul_mx(
+                        out=z[:],
+                        lhsT=xc[:, t, g, :].bitcast(FP8X4),
+                        lhsT_scale=xs[:, t, g, :],
+                        rhs=wc[:, g, cols].bitcast(FP8X4),
+                        rhs_scale=ws[:, g, cols],
+                        start=(g == 0),
+                        stop=(g == NG - 1),
+                    )
+                nc.vector.scalar_tensor_tensor(
+                    out=v[:, cols], in0=z[:], scalar=TURN, in1=b_sb[:, cols], op0=ALU.mult, op1=ALU.add
+                )
+            kk = epi.tile([NP, N], F32, name="kk")
+            nc.vector.tensor_scalar(out=kk[:], in0=v[:], scalar1=MAGIC, scalar2=MAGIC, op0=ALU.add, op1=ALU.subtract)
+            fr = epi.tile([NP, N], F32, name="fr")
+            nc.vector.tensor_tensor(out=fr[:], in0=v[:], in1=kk[:], op=ALU.subtract)
+            sn = epi.tile([NP, N], F32, name="sn")
+            nc.scalar.activation(out=sn[:], in_=fr[:], func=ACT.Sin, scale=2.0 * math.pi)
+            per = epi.tile([NP, N], F32, name="per")
+            nc.scalar.activation(out=per[:], in_=sn[:], func=ACT.Copy, scale=amp[:])
+            nc.sync.dma_start(out=out_view[:, t, K : K + N], in_=per[:])

@@ -6,6 +6,7 @@ from concourse.masks import make_identity
 
 F32 = mybir.dt.float32
 BF16 = mybir.dt.bfloat16
+I32 = mybir.dt.int32
 U32 = mybir.dt.uint32
 U8 = mybir.dt.uint8
 FP8X4 = mybir.dt.float8_e4m3fn_x4
@@ -20,9 +21,9 @@ K = 1024
 N = 1024
 NT = B // NP
 NG = K // 512
-NH = N // 512
+NJ = N // NP
+NHB = B // 512
 TURN = 1.0 / (2.0 * math.pi)
-MAGIC = 12582912.0
 GUARD = 1e-30
 PI_BELOW = 3.1415925025939941
 
@@ -32,165 +33,120 @@ def tile_time2vec_kernel(tc, x, W, P, w, p, sine_w, cosine_w, out):
     with ExitStack() as ctx:
         keep = ctx.enter_context(tc.tile_pool(name="keep", bufs=1))
         small = ctx.enter_context(tc.tile_pool(name="small", bufs=1))
-        linp = ctx.enter_context(tc.tile_pool(name="linp", bufs=4))
-        epi = ctx.enter_context(tc.tile_pool(name="epi", bufs=3))
+        linp = ctx.enter_context(tc.tile_pool(name="linp", bufs=8))
+        epi = ctx.enter_context(tc.tile_pool(name="epi", bufs=4))
         psum = ctx.enter_context(tc.psum_pool(name="psum", bufs=8))
 
         x_view = x.rearrange("(p t) k -> p t k", t=NT)
         out_view = out.rearrange("(p t) n -> p t n", t=NT)
-        w_view = W.rearrange("(g u q e) c -> g q u (e c)", g=NG, u=2, q=NP, e=2)
-
-        warm = small.tile([NP, 1], F32)
-        nc.vector.memset(warm[:], 0.0)
-        junk = small.tile([NP, 1], F32)
-        nc.scalar.activation(out=junk[:], in_=warm[:], func=ACT.Sin)
-        ones = keep.tile([NP, NP], BF16)
-        nc.vector.memset(ones[:], 1.0)
-        prow = keep.tile([NP, N], BF16)
-        nc.vector.memset(prow[:], 0.0)
-        ident = keep.tile([NP, NP], F32)
-        make_identity(nc, ident[:])
-
-        raw16 = small.tile([NP, 4, 16], BF16)
-        with nc.allow_non_contiguous_dma(reason="four scalars, one element a partition"):
-            for j, src in enumerate((w, p, cosine_w, sine_w)):
-                nc.scalar.dma_start(out=raw16[:, j, 0:1], in_=src.partition_broadcast(NP))
-        nc.scalar.dma_start(out=prow[0:1, :], in_=P.rearrange("(o n) -> o n", o=1))
-
-        x_sb = keep.tile([NP, NT, K], BF16)
-        w_raw = keep.tile([NP, NG, 4, N], BF16)
-
-        def load_x(j):
-            nc.sync.dma_start(out=x_sb[:, 2 * j : 2 * j + 2, :], in_=x_view[:, 2 * j : 2 * j + 2, :])
-
-        def load_w(g):
-            nc.sync.dma_start(
-                out=w_raw[:, g].rearrange("p (u e) c -> p u (e c)", u=2), in_=w_view[g]
-            )
-
-        load_x(0)
-        load_w(0)
-        load_x(1)
-        load_w(1)
-        load_x(2)
-        load_x(3)
-
-        pbs = []
-        for h in range(NH):
-            pb = psum.tile([NP, 512], F32, tag="bank", name="pb%d" % h)
-            nc.tensor.matmul(out=pb[:], lhsT=ones[:], rhs=prow[:, 512 * h : 512 * h + 512], start=True, stop=True)
-            pbs.append(pb)
+        w_view = W.rearrange("(g u q e) c -> g u q (e c)", g=NG, u=2, q=NP, e=2)
 
         def col(name):
             return small.tile([NP, 1], F32, name=name)
 
+        raw16 = small.tile([NP, 4, 16], BF16)
+        prow = keep.tile([NP, NP], BF16)
+        warm = small.tile([NP, 1], F32)
+        junk = small.tile([NP, 1], F32)
+        ident = keep.tile([NP, NP], F32)
+        identb = keep.tile([NP, NP], BF16)
+        x_sb = keep.tile([NP, NT, K], BF16)
+        w_raw = keep.tile([NP, NG, 4, N], BF16)
         sc32 = small.tile([NP, 4], F32)
-        nc.vector.tensor_scalar(out=sc32[:], in0=raw16[:, :, 0], scalar1=GUARD, scalar2=None, op0=ALU.add)
         w32 = sc32[:, 0:1]
         p32 = sc32[:, 1:2]
+        sc32g = small.tile([NP, 2], F32)
         sg2 = col("sg2")
-        nc.vector.tensor_scalar(out=sg2[:], in0=sc32[:, 3:4], scalar1=0.0, scalar2=2.0, op0=ALU.is_ge, op1=ALU.mult)
         cs1 = small.tile([NP, 2], F32)
-        nc.vector.scalar_tensor_tensor(
-            out=cs1[:], in0=sc32[:, 2:4], scalar=sg2[:], in1=sc32[:, 2:4], op0=ALU.mult, op1=ALU.subtract
-        )
         c1 = cs1[:, 0:1]
         s1 = cs1[:, 1:2]
         absc = col("absc")
-        nc.vector.scalar_tensor_tensor(out=absc[:], in0=c1, scalar=-1.0, in1=c1, op0=ALU.mult, op1=ALU.max)
         den = col("den")
-        nc.vector.tensor_scalar(out=den[:], in0=absc[:], scalar1=s1, scalar2=None, op0=ALU.add)
         rden = col("rden")
-        nc.vector.reciprocal(out=rden[:], in_=den[:])
         ang = small.tile([NP, 2], F32)
-        nc.vector.tensor_scalar(
-            out=ang[:, 0:1], in0=c1, scalar1=rden[:], scalar2=0.5 * math.pi, op0=ALU.mult, op1=ALU.mult
-        )
-        nc.vector.tensor_scalar(
-            out=ang[:, 1:2], in0=ang[:, 0:1], scalar1=0.5 * math.pi, scalar2=PI_BELOW, op0=ALU.add, op1=ALU.min
-        )
         sico = small.tile([NP, 2], F32)
-        nc.scalar.activation(out=sico[:], in_=ang[:], func=ACT.Sin)
         tsin = small.tile([NP, 2], F32)
-        nc.vector.tensor_scalar(out=tsin[:], in0=cs1[:], scalar1=sico[:, 0:1], scalar2=None, op0=ALU.mult)
         dd = col("dd")
-        nc.vector.scalar_tensor_tensor(
-            out=dd[:], in0=s1, scalar=sico[:, 1:2], in1=tsin[:, 0:1], op0=ALU.mult, op1=ALU.add
-        )
         nn = col("nn")
-        nc.vector.scalar_tensor_tensor(
-            out=nn[:], in0=c1, scalar=sico[:, 1:2], in1=tsin[:, 1:2], op0=ALU.mult, op1=ALU.subtract
-        )
         rdd = col("rdd")
-        nc.vector.reciprocal(out=rdd[:], in_=dd[:])
         tau = col("tau")
-        nc.vector.tensor_scalar(out=tau[:], in0=nn[:], scalar1=rdd[:], scalar2=None, op0=ALU.mult)
         tau2 = col("tau2")
-        nc.vector.tensor_scalar(out=tau2[:], in0=tau[:], scalar1=tau[:], scalar2=None, op0=ALU.mult)
-        tauc = col("tauc")
-        nc.vector.tensor_scalar(out=tauc[:], in0=tau[:], scalar1=TURN, scalar2=None, op0=ALU.mult)
-        phi0c = col("phi0c")
-        nc.vector.tensor_scalar(out=phi0c[:], in0=ang[:, 0:1], scalar1=TURN, scalar2=None, op0=ALU.mult)
         h1 = col("h1")
-        nc.vector.tensor_scalar(out=h1[:], in0=tau2[:], scalar1=-1.0 / 7.0, scalar2=0.2, op0=ALU.mult, op1=ALU.add)
         h2 = col("h2")
-        nc.vector.tensor_scalar(out=h2[:], in0=h1[:], scalar1=tau2[:], scalar2=-1.0 / 3.0, op0=ALU.mult, op1=ALU.add)
         h3 = col("h3")
-        nc.vector.tensor_scalar(out=h3[:], in0=h2[:], scalar1=tau2[:], scalar2=1.0, op0=ALU.mult, op1=ALU.add)
-        phit = col("phit")
-        nc.vector.tensor_scalar(out=phit[:], in0=h3[:], scalar1=tauc[:], scalar2=phi0c[:], op0=ALU.mult, op1=ALU.add)
+        phi = col("phi")
+        beta = small.tile([NP, NJ], F32)
+        bturn = small.tile([NP, NJ], F32)
         g1 = col("g1")
-        nc.vector.tensor_scalar(out=g1[:], in0=tau2[:], scalar1=1.0 / 16.0, scalar2=-0.125, op0=ALU.mult, op1=ALU.add)
         g2 = col("g2")
-        nc.vector.tensor_scalar(out=g2[:], in0=g1[:], scalar1=tau2[:], scalar2=0.5, op0=ALU.mult, op1=ALU.add)
         g3 = col("g3")
-        nc.vector.tensor_scalar(out=g3[:], in0=g2[:], scalar1=tau2[:], scalar2=1.0, op0=ALU.mult, op1=ALU.add)
         dsg = col("dsg")
-        nc.vector.scalar_tensor_tensor(out=dsg[:], in0=dd[:], scalar=sg2[:], in1=dd[:], op0=ALU.mult, op1=ALU.subtract)
         amp = col("amp")
-        nc.vector.tensor_scalar(out=amp[:], in0=g3[:], scalar1=dsg[:], scalar2=None, op0=ALU.mult)
-
-        b_sb = keep.tile([NP, N], F32)
-        for h in range(NH):
-            nc.scalar.activation(
-                out=b_sb[:, 512 * h : 512 * h + 512], in_=pbs[h][:], func=ACT.Identity, scale=TURN, bias=phit[:]
-            )
-
-        xg = keep.tile([NP, NT, K], BF16, align_bytes=64)
-        xc = keep.tile([NP, NT, NG, NP], U32, align_bytes=64)
-        xs = keep.tile([NP, NT, NG, NP], U8, align_bytes=64)
+        xg = keep.tile([NP, NG, NT, 512], BF16, align_bytes=64)
+        xc = keep.tile([NP, NG, B], U32, align_bytes=64)
+        xs = keep.tile([NP, NG, B], U8, align_bytes=64)
         wg = keep.tile([NP, NG, N, 4], BF16, align_bytes=64)
         wc = keep.tile([NP, NG, N], U32, align_bytes=64)
         ws = keep.tile([NP, NG, N], U8, align_bytes=64)
+        stages = [keep.tile([NP, 4, N], F32, name="stage%d" % hb) for hb in range(NHB)]
+        live = {}
+        scalars = (w, p, cosine_w, sine_w)
 
-        def x_tile(t):
+        def load_scalar(j):
+            with nc.allow_non_contiguous_dma(reason="one element a partition"):
+                nc.scalar.dma_start(out=raw16[:, j, 0:1], in_=scalars[j].partition_broadcast(NP))
+
+        def load_x(j):
+            nc.sync.dma_start(out=x_sb[:, 2 * j : 2 * j + 2, :], in_=x_view[:, 2 * j : 2 * j + 2, :])
+
+        def load_w(g, u):
+            nc.sync.dma_start(
+                out=w_raw[:, g, 2 * u : 2 * u + 2, :].rearrange("p e c -> p (e c)"), in_=w_view[g, u]
+            )
+
+        def x_transpose(t):
             xt = psum.tile([NP, 4, NP], F32, tag="bank", name="xt%d" % t)
             xw = x_sb[:, t, :].bitcast(F32)
             for j in range(4):
                 nc.tensor.transpose(out=xt[:, j, :], in_=xw[:, NP * j : NP * j + NP], identity=ident[:])
-            nc.scalar.copy(
-                out=xg[:, t, :].bitcast(F32).rearrange("p (g b u) -> p g b u", g=NG, b=NP, u=2),
-                in_=xt[:].rearrange("p (g u) b -> p g b u", g=NG, u=2),
-            )
+            live[("xt", t)] = xt
 
-        def x_quant(t):
+        def x_copy(t, eng):
+            dst = xg[:, :, t, :].bitcast(F32).rearrange("p g (b u) -> p g b u", u=2)
+            src = live[("xt", t)][:].rearrange("p (g u) b -> p g b u", g=NG, u=2)
+            if eng == "S":
+                nc.scalar.copy(out=dst, in_=src)
+            else:
+                nc.vector.tensor_copy(out=dst, in_=src)
+
+        def x_quant(g, jj):
             nc.vector.quantize_mx(
-                out=xc[:, t].rearrange("p g b -> p (g b)").bitcast(FP8X4),
-                scales=xs[:, t].rearrange("p g b -> p (g b)"),
-                in_=xg[:, t, :],
+                out=xc[:, g, 256 * jj : 256 * jj + 256].bitcast(FP8X4),
+                scales=xs[:, g, 256 * jj : 256 * jj + 256],
+                in_=xg[:, g, 2 * jj : 2 * jj + 2, :].rearrange("p t c -> p (t c)"),
             )
 
-        def linear(t):
+        def linear(t, eng):
             lin = linp.tile([NP, K], F32, name="lin")
-            nc.scalar.activation(out=lin[:], in_=x_sb[:, t, :], func=ACT.Identity, scale=w32, bias=p32)
-            nc.sync.dma_start(out=out_view[:, t, 0:K], in_=lin[:])
+            if eng == "S":
+                nc.scalar.activation(out=lin[:], in_=x_sb[:, t, :], func=ACT.Identity, scale=w32, bias=p32)
+            elif eng == "G":
+                nc.gpsimd.tensor_scalar(out=lin[:], in0=x_sb[:, t, :], scalar1=sc32g[:, 0:1], scalar2=sc32g[:, 1:2], op0=ALU.mult, op1=ALU.add)
+            else:
+                nc.vector.tensor_scalar(out=lin[:], in0=x_sb[:, t, :], scalar1=w32, scalar2=p32, op0=ALU.mult, op1=ALU.add)
+            live[("lin", t)] = lin
 
-        def w_regroup(g, h):
+        def store_linear(t):
+            nc.sync.dma_start(out=out_view[:, t, 0:K], in_=live[("lin", t)][:])
+
+        def w_regroup(g, h, eng):
             cols = slice(512 * h, 512 * h + 512)
-            nc.vector.tensor_copy(
-                out=wg[:, g, cols, :].rearrange("p (c i) t -> p c t i", i=4),
-                in_=w_raw[:, g, :, cols].rearrange("p t (c i) -> p c t i", i=4),
-            )
+            dst = wg[:, g, cols, :].rearrange("p (c i) t -> p c t i", i=4)
+            src = w_raw[:, g, :, cols].rearrange("p t (c i) -> p c t i", i=4)
+            if eng == "S":
+                nc.scalar.copy(out=dst, in_=src)
+            else:
+                nc.vector.tensor_copy(out=dst, in_=src)
 
         def w_quant(g, h):
             cols = slice(512 * h, 512 * h + 512)
@@ -200,57 +156,258 @@ def tile_time2vec_kernel(tc, x, W, P, w, p, sine_w, cosine_w, out):
                 in_=wg[:, g, cols, :].rearrange("p c t -> p (c t)"),
             )
 
-        x_tile(0)
-        x_tile(1)
-        w_regroup(0, 0)
-        w_regroup(0, 1)
-        x_quant(0)
-        w_quant(0, 0)
-        x_quant(1)
-        w_quant(0, 1)
-        linear(0)
-        linear(1)
-        x_tile(2)
-        x_tile(3)
-        w_regroup(1, 0)
-        w_regroup(1, 1)
-        x_quant(2)
-        w_quant(1, 0)
-        x_quant(3)
-        w_quant(1, 1)
-        linear(2)
-        linear(3)
-        for t in range(4, NT):
-            x_tile(t)
-        for t in range(4, NT):
-            x_quant(t)
-        for t in range(4, NT):
-            linear(t)
-
-        for t in range(NT):
-            v = epi.tile([NP, N], F32, name="v")
-            for h in range(NH):
-                cols = slice(512 * h, 512 * h + 512)
-                z = psum.tile([NP, 512], F32, tag="bank", name="z")
-                for g in range(NG):
-                    nc.tensor.matmul_mx(
-                        out=z[:],
-                        lhsT=xc[:, t, g, :].bitcast(FP8X4),
-                        lhsT_scale=xs[:, t, g, :],
-                        rhs=wc[:, g, cols].bitcast(FP8X4),
-                        rhs_scale=ws[:, g, cols],
-                        start=(g == 0),
-                        stop=(g == NG - 1),
-                    )
-                nc.vector.scalar_tensor_tensor(
-                    out=v[:, cols], in0=z[:], scalar=TURN, in1=b_sb[:, cols], op0=ALU.mult, op1=ALU.add
+        def mm(hb, j):
+            z = psum.tile([NP, 512], F32, tag="bank", name="z")
+            for g in range(NG):
+                nc.tensor.matmul_mx(
+                    out=z[:],
+                    lhsT=wc[:, g, NP * j : NP * j + NP].bitcast(FP8X4),
+                    lhsT_scale=ws[:, g, NP * j : NP * j + NP],
+                    rhs=xc[:, g, 512 * hb : 512 * hb + 512].bitcast(FP8X4),
+                    rhs_scale=xs[:, g, 512 * hb : 512 * hb + 512],
+                    start=(g == 0),
+                    stop=(g == NG - 1),
                 )
-            kk = epi.tile([NP, N], F32, name="kk")
-            nc.vector.tensor_scalar(out=kk[:], in0=v[:], scalar1=MAGIC, scalar2=MAGIC, op0=ALU.add, op1=ALU.subtract)
-            fr = epi.tile([NP, N], F32, name="fr")
-            nc.vector.tensor_tensor(out=fr[:], in0=v[:], in1=kk[:], op=ALU.subtract)
-            sn = epi.tile([NP, N], F32, name="sn")
-            nc.scalar.activation(out=sn[:], in_=fr[:], func=ACT.Sin, scale=2.0 * math.pi)
-            per = epi.tile([NP, N], F32, name="per")
-            nc.scalar.activation(out=per[:], in_=sn[:], func=ACT.Copy, scale=amp[:])
-            nc.sync.dma_start(out=out_view[:, t, K : K + N], in_=per[:])
+            live[("z", hb, j)] = z
+
+        def t1(hb, j):
+            ki = epi.tile([NP, 512], I32, name="ki")
+            nc.vector.tensor_scalar(
+                out=ki[:], in0=live[("z", hb, j)][:], scalar1=TURN, scalar2=bturn[:, j : j + 1], op0=ALU.mult, op1=ALU.add
+            )
+            live[("k", hb, j)] = ki
+
+        def t2(hb, j):
+            fr = epi.tile([NP, 512], F32, name="fr")
+            nc.vector.scalar_tensor_tensor(
+                out=fr[:], in0=live[("z", hb, j)][:], scalar=TURN, in1=live[("k", hb, j)][:], op0=ALU.mult, op1=ALU.subtract
+            )
+            live[("f", hb, j)] = fr
+
+        def sin(hb, j):
+            sn = epi.tile([NP, 512], F32, name="sn")
+            nc.scalar.activation(
+                out=sn[:], in_=live[("f", hb, j)][:], func=ACT.Sin, scale=2.0 * math.pi, bias=beta[:, j : j + 1]
+            )
+            live[("s", hb, j)] = sn
+
+        def tr(hb, j):
+            ob = psum.tile([NP, 4, NP], F32, tag="bank", name="ob")
+            sn = live[("s", hb, j)]
+            for i in range(4):
+                nc.tensor.transpose(out=ob[:, i, :], in_=sn[:, NP * i : NP * i + NP], identity=ident[:])
+            live[("o", hb, j)] = ob
+
+        def outc(hb, j, eng):
+            dst = stages[hb][:, :, NP * j : NP * j + NP]
+            if eng == "S":
+                nc.scalar.activation(out=dst, in_=live[("o", hb, j)][:], func=ACT.Copy, scale=amp[:])
+            else:
+                nc.vector.tensor_scalar(out=dst, in0=live[("o", hb, j)][:], scalar1=amp[:], scalar2=None, op0=ALU.mult)
+
+        def store(hb, j0, j1):
+            nc.sync.dma_start(
+                out=out_view[:, 4 * hb : 4 * hb + 4, K + NP * j0 : K + NP * j1], in_=stages[hb][:, :, NP * j0 : NP * j1]
+            )
+
+        ctx.enter_context(tc.manual_schedule())
+        nc.vector.memset(prow[:], 0.0)
+        nc.vector.memset(warm[:], 0.0)
+        pt = psum.tile([NP, NP], BF16, tag="bank", name="pt")
+        load_scalar(0)
+        load_w(0, 0)
+        make_identity(nc, ident[:])
+        load_scalar(1)
+        load_w(0, 1)
+        load_scalar(2)
+        load_x(0)
+        load_scalar(3)
+        load_w(1, 0)
+        nc.scalar.dma_start(out=prow[0:NJ, :], in_=P.rearrange("(j n) -> j n", n=NP))
+        load_w(1, 1)
+        nc.scalar.activation(out=junk[:], in_=warm[:], func=ACT.Sin)
+        load_x(1)
+        load_x(2)
+        load_x(3)
+        nc.gpsimd.tensor_copy(out=identb[:], in_=ident[:])
+        nc.vector.tensor_scalar(out=sc32[:], in0=raw16[:, :, 0], scalar1=GUARD, scalar2=None, op0=ALU.add)
+        nc.tensor.transpose(out=pt[:], in_=prow[:], identity=identb[:])
+        nc.vector.tensor_scalar(out=sg2[:], in0=sc32[:, 3:4], scalar1=0.0, scalar2=2.0, op0=ALU.is_ge, op1=ALU.mult)
+        nc.vector.scalar_tensor_tensor(out=cs1[:], in0=sc32[:, 2:4], scalar=sg2[:], in1=sc32[:, 2:4], op0=ALU.mult, op1=ALU.subtract)
+        nc.vector.scalar_tensor_tensor(out=absc[:], in0=c1, scalar=-1.0, in1=c1, op0=ALU.mult, op1=ALU.max)
+        nc.vector.tensor_scalar(out=den[:], in0=absc[:], scalar1=s1, scalar2=None, op0=ALU.add)
+        nc.vector.reciprocal(out=rden[:], in_=den[:])
+        nc.vector.tensor_scalar(out=ang[:, 0:1], in0=c1, scalar1=rden[:], scalar2=0.5 * math.pi, op0=ALU.mult, op1=ALU.mult)
+        nc.vector.tensor_scalar(out=ang[:, 1:2], in0=ang[:, 0:1], scalar1=0.5 * math.pi, scalar2=PI_BELOW, op0=ALU.add, op1=ALU.min)
+        w_regroup(0, 0, "V")
+        nc.scalar.activation(out=sico[:], in_=ang[:], func=ACT.Sin)
+        nc.vector.tensor_scalar(out=tsin[:], in0=cs1[:], scalar1=sico[:, 0:1], scalar2=None, op0=ALU.mult)
+        x_transpose(0)
+        w_regroup(0, 1, "V")
+        x_transpose(1)
+        x_copy(0, "S")
+        x_copy(1, "S")
+        nc.vector.scalar_tensor_tensor(out=dd[:], in0=s1, scalar=sico[:, 1:2], in1=tsin[:, 0:1], op0=ALU.mult, op1=ALU.add)
+        w_quant(0, 0)
+        linear(0, "S")
+        nc.vector.scalar_tensor_tensor(out=nn[:], in0=c1, scalar=sico[:, 1:2], in1=tsin[:, 1:2], op0=ALU.mult, op1=ALU.subtract)
+        w_quant(0, 1)
+        nc.vector.reciprocal(out=rdd[:], in_=dd[:])
+        x_quant(0, 0)
+        linear(1, "S")
+        nc.vector.tensor_scalar(out=tau[:], in0=nn[:], scalar1=rdd[:], scalar2=None, op0=ALU.mult)
+        store_linear(0)
+        x_quant(1, 0)
+        nc.vector.tensor_scalar(out=tau2[:], in0=tau[:], scalar1=tau[:], scalar2=None, op0=ALU.mult)
+        w_regroup(1, 0, "V")
+        x_transpose(2)
+        x_transpose(3)
+        store_linear(1)
+        x_copy(2, "S")
+        nc.vector.tensor_scalar(out=h1[:], in0=tau2[:], scalar1=-1.0 / 7.0, scalar2=0.2, op0=ALU.mult, op1=ALU.add)
+        w_regroup(1, 1, "V")
+        x_copy(3, "S")
+        x_transpose(4)
+        x_transpose(5)
+        linear(2, "S")
+        nc.vector.tensor_scalar(out=h2[:], in0=h1[:], scalar1=tau2[:], scalar2=-1.0 / 3.0, op0=ALU.mult, op1=ALU.add)
+        w_quant(1, 0)
+        x_transpose(6)
+        nc.vector.tensor_scalar(out=h3[:], in0=h2[:], scalar1=tau2[:], scalar2=1.0, op0=ALU.mult, op1=ALU.add)
+        linear(3, "S")
+        x_transpose(7)
+        x_quant(0, 1)
+        store_linear(2)
+        nc.vector.tensor_scalar(out=phi[:], in0=h3[:], scalar1=tau[:], scalar2=ang[:, 0:1], op0=ALU.mult, op1=ALU.add)
+        x_quant(1, 1)
+        nc.vector.tensor_scalar(out=beta[:], in0=pt[:, 0:NJ], scalar1=phi[:], scalar2=None, op0=ALU.add)
+        w_quant(1, 1)
+        mm(0, 0)
+        x_copy(4, "S")
+        store_linear(3)
+        nc.vector.tensor_scalar(out=bturn[:], in0=pt[:, 0:NJ], scalar1=phi[:], scalar2=TURN, op0=ALU.add, op1=ALU.mult)
+        nc.vector.tensor_scalar(out=g1[:], in0=tau2[:], scalar1=1.0 / 16.0, scalar2=-0.125, op0=ALU.mult, op1=ALU.add)
+        mm(0, 1)
+        x_copy(5, "S")
+        nc.vector.tensor_scalar(out=g2[:], in0=g1[:], scalar1=tau2[:], scalar2=0.5, op0=ALU.mult, op1=ALU.add)
+        nc.vector.tensor_scalar(out=g3[:], in0=g2[:], scalar1=tau2[:], scalar2=1.0, op0=ALU.mult, op1=ALU.add)
+        nc.vector.scalar_tensor_tensor(out=dsg[:], in0=dd[:], scalar=sg2[:], in1=dd[:], op0=ALU.mult, op1=ALU.subtract)
+        x_copy(6, "S")
+        mm(0, 2)
+        nc.vector.tensor_scalar(out=amp[:], in0=g3[:], scalar1=dsg[:], scalar2=None, op0=ALU.mult)
+        nc.vector.tensor_copy(out=sc32g[:], in_=sc32[:, 0:2])
+        t1(0, 0)
+        linear(4, "G")
+        x_copy(7, "S")
+        mm(0, 3)
+        t1(0, 1)
+        mm(0, 4)
+        t2(0, 0)
+        linear(5, "G")
+        store_linear(4)
+        t1(0, 2)
+        sin(0, 0)
+        t2(0, 1)
+        linear(6, "G")
+        tr(0, 0)
+        store_linear(5)
+        x_quant(0, 2)
+        sin(0, 1)
+        mm(0, 5)
+        t1(0, 3)
+        outc(0, 0, "S")
+        tr(0, 1)
+        linear(7, "G")
+        t2(0, 2)
+        store_linear(6)
+        mm(0, 6)
+        x_quant(1, 2)
+        sin(0, 2)
+        t1(0, 4)
+        outc(0, 1, "S")
+        store_linear(7)
+        tr(0, 2)
+        t2(0, 3)
+        mm(0, 7)
+        store(0, 0, 2)
+        x_quant(0, 3)
+        sin(0, 3)
+        t1(0, 5)
+        outc(0, 2, "S")
+        tr(0, 3)
+        t2(0, 4)
+        x_quant(1, 3)
+        sin(0, 4)
+        t1(0, 6)
+        mm(1, 0)
+        outc(0, 3, "S")
+        t2(0, 5)
+        tr(0, 4)
+        store(0, 2, 4)
+        t1(0, 7)
+        mm(1, 1)
+        sin(0, 5)
+        t2(0, 6)
+        outc(0, 4, "S")
+        tr(0, 5)
+        t1(1, 0)
+        sin(0, 6)
+        mm(1, 2)
+        t2(0, 7)
+        outc(0, 5, "S")
+        tr(0, 6)
+        t1(1, 1)
+        sin(0, 7)
+        mm(1, 3)
+        store(0, 4, 6)
+        t2(1, 0)
+        outc(0, 6, "S")
+        tr(0, 7)
+        t1(1, 2)
+        sin(1, 0)
+        mm(1, 4)
+        t2(1, 1)
+        outc(0, 7, "S")
+        tr(1, 0)
+        t1(1, 3)
+        sin(1, 1)
+        mm(1, 5)
+        store(0, 6, 8)
+        t2(1, 2)
+        outc(1, 0, "S")
+        tr(1, 1)
+        t1(1, 4)
+        sin(1, 2)
+        mm(1, 6)
+        t2(1, 3)
+        outc(1, 1, "S")
+        tr(1, 2)
+        t1(1, 5)
+        sin(1, 3)
+        mm(1, 7)
+        store(1, 0, 2)
+        t2(1, 4)
+        outc(1, 2, "S")
+        tr(1, 3)
+        t1(1, 6)
+        sin(1, 4)
+        t2(1, 5)
+        outc(1, 3, "S")
+        tr(1, 4)
+        t1(1, 7)
+        sin(1, 5)
+        store(1, 2, 4)
+        t2(1, 6)
+        outc(1, 4, "S")
+        tr(1, 5)
+        t2(1, 7)
+        sin(1, 6)
+        outc(1, 5, "S")
+        tr(1, 6)
+        sin(1, 7)
+        store(1, 4, 6)
+        outc(1, 6, "S")
+        tr(1, 7)
+        store(1, 6, 7)
+        outc(1, 7, "S")
+        store(1, 7, 8)

@@ -39,7 +39,8 @@ def tile_time2vec_kernel(tc, x, W, P, w, p, sine_w, cosine_w, out):
 
         x_view = x.rearrange("(p t) k -> p t k", t=NT)
         out_view = out.rearrange("(p t) n -> p t n", t=NT)
-        w_view = W.rearrange("(g u q e) c -> g u q (e c)", g=NG, u=2, q=NP, e=2)
+        w_view0 = W.rearrange("(g u q e) c -> g u q e c", g=NG, u=2, q=NP, e=2)
+        w_view1 = W.rearrange("(a q e) c -> e q a c", a=2 * NG, q=NP, e=2)
 
         def col(name):
             return small.tile([NP, 1], F32, name=name)
@@ -99,9 +100,12 @@ def tile_time2vec_kernel(tc, x, W, P, w, p, sine_w, cosine_w, out):
         def load_x(j):
             nc.sync.dma_start(out=x_sb[:, 2 * j : 2 * j + 2, :], in_=x_view[:, 2 * j : 2 * j + 2, :])
 
-        def load_w(g, u):
+        def load_w0(g, u):
+            nc.sync.dma_start(out=w_raw[:, g, 2 * u : 2 * u + 2, 0:512], in_=w_view0[g, u][:, :, 0:512])
+
+        def load_w1(e):
             nc.sync.dma_start(
-                out=w_raw[:, g, 2 * u : 2 * u + 2, :].rearrange("p e c -> p (e c)"), in_=w_view[g, u]
+                out=w_raw[:].rearrange("p g (u e) c -> p (g u) e c", e=2)[:, :, e, 512:N], in_=w_view1[e][:, :, 512:N]
             )
 
         def x_transpose(t):
@@ -145,6 +149,8 @@ def tile_time2vec_kernel(tc, x, W, P, w, p, sine_w, cosine_w, out):
             src = w_raw[:, g, :, cols].rearrange("p t (c i) -> p c t i", i=4)
             if eng == "S":
                 nc.scalar.copy(out=dst, in_=src)
+            elif eng == "G":
+                nc.gpsimd.tensor_scalar(out=dst, in0=src, scalar1=1.0, scalar2=0.0, op0=ALU.mult, op1=ALU.add)
             else:
                 nc.vector.tensor_copy(out=dst, in_=src)
 
@@ -215,199 +221,200 @@ def tile_time2vec_kernel(tc, x, W, P, w, p, sine_w, cosine_w, out):
         nc.vector.memset(warm[:], 0.0)
         pt = psum.tile([NP, NP], BF16, tag="bank", name="pt")
         load_scalar(0)
-        load_w(0, 0)
+        load_w0(0, 0)
         make_identity(nc, ident[:])
         load_scalar(1)
-        load_w(0, 1)
+        load_w0(0, 1)
         load_scalar(2)
         load_x(0)
         load_scalar(3)
-        load_w(1, 0)
+        load_w0(1, 0)
         nc.scalar.dma_start(out=prow[0:NJ, :], in_=P.rearrange("(j n) -> j n", n=NP))
-        load_w(1, 1)
+        load_w0(1, 1)
         nc.scalar.activation(out=junk[:], in_=warm[:], func=ACT.Sin)
         load_x(1)
         load_x(2)
         load_x(3)
+        load_w1(0)
+        load_w1(1)
         nc.gpsimd.tensor_copy(out=identb[:], in_=ident[:])
         nc.vector.tensor_scalar(out=sc32[:], in0=raw16[:, :, 0], scalar1=GUARD, scalar2=None, op0=ALU.add)
         nc.tensor.transpose(out=pt[:], in_=prow[:], identity=identb[:])
         nc.vector.tensor_scalar(out=sg2[:], in0=sc32[:, 3:4], scalar1=0.0, scalar2=2.0, op0=ALU.is_ge, op1=ALU.mult)
         nc.vector.scalar_tensor_tensor(out=cs1[:], in0=sc32[:, 2:4], scalar=sg2[:], in1=sc32[:, 2:4], op0=ALU.mult, op1=ALU.subtract)
         nc.vector.scalar_tensor_tensor(out=absc[:], in0=c1, scalar=-1.0, in1=c1, op0=ALU.mult, op1=ALU.max)
-        nc.vector.tensor_scalar(out=den[:], in0=absc[:], scalar1=s1, scalar2=None, op0=ALU.add)
-        nc.vector.reciprocal(out=rden[:], in_=den[:])
-        nc.vector.tensor_scalar(out=ang[:, 0:1], in0=c1, scalar1=rden[:], scalar2=0.5 * math.pi, op0=ALU.mult, op1=ALU.mult)
-        nc.vector.tensor_scalar(out=ang[:, 1:2], in0=ang[:, 0:1], scalar1=0.5 * math.pi, scalar2=PI_BELOW, op0=ALU.add, op1=ALU.min)
         w_regroup(0, 0, "V")
-        nc.scalar.activation(out=sico[:], in_=ang[:], func=ACT.Sin)
-        nc.vector.tensor_scalar(out=tsin[:], in0=cs1[:], scalar1=sico[:, 0:1], scalar2=None, op0=ALU.mult)
+        nc.vector.tensor_scalar(out=den[:], in0=absc[:], scalar1=s1, scalar2=None, op0=ALU.add)
         x_transpose(0)
-        w_regroup(0, 1, "V")
+        nc.vector.reciprocal(out=rden[:], in_=den[:])
+        w_quant(0, 0)
         x_transpose(1)
         x_copy(0, "S")
+        nc.vector.tensor_scalar(out=ang[:, 0:1], in0=c1, scalar1=rden[:], scalar2=0.5 * math.pi, op0=ALU.mult, op1=ALU.mult)
+        nc.vector.tensor_scalar(out=ang[:, 1:2], in0=ang[:, 0:1], scalar1=0.5 * math.pi, scalar2=PI_BELOW, op0=ALU.add, op1=ALU.min)
         x_copy(1, "S")
-        nc.vector.scalar_tensor_tensor(out=dd[:], in0=s1, scalar=sico[:, 1:2], in1=tsin[:, 0:1], op0=ALU.mult, op1=ALU.add)
-        w_quant(0, 0)
-        linear(0, "S")
-        nc.vector.scalar_tensor_tensor(out=nn[:], in0=c1, scalar=sico[:, 1:2], in1=tsin[:, 1:2], op0=ALU.mult, op1=ALU.subtract)
-        w_quant(0, 1)
-        nc.vector.reciprocal(out=rdd[:], in_=dd[:])
-        x_quant(0, 0)
-        linear(1, "S")
-        nc.vector.tensor_scalar(out=tau[:], in0=nn[:], scalar1=rdd[:], scalar2=None, op0=ALU.mult)
-        store_linear(0)
-        x_quant(1, 0)
-        nc.vector.tensor_scalar(out=tau2[:], in0=tau[:], scalar1=tau[:], scalar2=None, op0=ALU.mult)
         w_regroup(1, 0, "V")
+        nc.scalar.activation(out=sico[:], in_=ang[:], func=ACT.Sin)
+        nc.vector.tensor_scalar(out=tsin[:], in0=cs1[:], scalar1=sico[:, 0:1], scalar2=None, op0=ALU.mult)
         x_transpose(2)
+        nc.vector.scalar_tensor_tensor(out=dd[:], in0=s1, scalar=sico[:, 1:2], in1=tsin[:, 0:1], op0=ALU.mult, op1=ALU.add)
+        nc.vector.scalar_tensor_tensor(out=nn[:], in0=c1, scalar=sico[:, 1:2], in1=tsin[:, 1:2], op0=ALU.mult, op1=ALU.subtract)
+        x_quant(0, 0)
         x_transpose(3)
-        store_linear(1)
         x_copy(2, "S")
-        nc.vector.tensor_scalar(out=h1[:], in0=tau2[:], scalar1=-1.0 / 7.0, scalar2=0.2, op0=ALU.mult, op1=ALU.add)
-        w_regroup(1, 1, "V")
+        nc.vector.reciprocal(out=rdd[:], in_=dd[:])
+        nc.vector.tensor_scalar(out=tau[:], in0=nn[:], scalar1=rdd[:], scalar2=None, op0=ALU.mult)
+        w_quant(1, 0)
         x_copy(3, "S")
         x_transpose(4)
+        nc.vector.tensor_scalar(out=tau2[:], in0=tau[:], scalar1=tau[:], scalar2=None, op0=ALU.mult)
         x_transpose(5)
-        linear(2, "S")
+        x_copy(4, "S")
+        nc.vector.tensor_scalar(out=h1[:], in0=tau2[:], scalar1=-1.0 / 7.0, scalar2=0.2, op0=ALU.mult, op1=ALU.add)
+        x_quant(1, 0)
         nc.vector.tensor_scalar(out=h2[:], in0=h1[:], scalar1=tau2[:], scalar2=-1.0 / 3.0, op0=ALU.mult, op1=ALU.add)
-        w_quant(1, 0)
+        x_copy(5, "S")
         x_transpose(6)
         nc.vector.tensor_scalar(out=h3[:], in0=h2[:], scalar1=tau2[:], scalar2=1.0, op0=ALU.mult, op1=ALU.add)
-        linear(3, "S")
-        x_transpose(7)
         x_quant(0, 1)
-        store_linear(2)
+        x_transpose(7)
         nc.vector.tensor_scalar(out=phi[:], in0=h3[:], scalar1=tau[:], scalar2=ang[:, 0:1], op0=ALU.mult, op1=ALU.add)
         x_quant(1, 1)
+        x_copy(6, "S")
         nc.vector.tensor_scalar(out=beta[:], in0=pt[:, 0:NJ], scalar1=phi[:], scalar2=None, op0=ALU.add)
-        w_quant(1, 1)
-        mm(0, 0)
-        x_copy(4, "S")
-        store_linear(3)
         nc.vector.tensor_scalar(out=bturn[:], in0=pt[:, 0:NJ], scalar1=phi[:], scalar2=TURN, op0=ALU.add, op1=ALU.mult)
+        mm(0, 0)
+        x_quant(0, 2)
+        x_copy(7, "S")
+        nc.vector.tensor_copy(out=sc32g[:], in_=sc32[:, 0:2])
         nc.vector.tensor_scalar(out=g1[:], in0=tau2[:], scalar1=1.0 / 16.0, scalar2=-0.125, op0=ALU.mult, op1=ALU.add)
+        x_quant(1, 2)
+        linear(3, "G")
         mm(0, 1)
-        x_copy(5, "S")
+        linear(0, "S")
         nc.vector.tensor_scalar(out=g2[:], in0=g1[:], scalar1=tau2[:], scalar2=0.5, op0=ALU.mult, op1=ALU.add)
         nc.vector.tensor_scalar(out=g3[:], in0=g2[:], scalar1=tau2[:], scalar2=1.0, op0=ALU.mult, op1=ALU.add)
-        nc.vector.scalar_tensor_tensor(out=dsg[:], in0=dd[:], scalar=sg2[:], in1=dd[:], op0=ALU.mult, op1=ALU.subtract)
-        x_copy(6, "S")
+        x_quant(0, 3)
         mm(0, 2)
+        nc.vector.scalar_tensor_tensor(out=dsg[:], in0=dd[:], scalar=sg2[:], in1=dd[:], op0=ALU.mult, op1=ALU.subtract)
         nc.vector.tensor_scalar(out=amp[:], in0=g3[:], scalar1=dsg[:], scalar2=None, op0=ALU.mult)
-        nc.vector.tensor_copy(out=sc32g[:], in_=sc32[:, 0:2])
-        t1(0, 0)
-        linear(4, "G")
-        x_copy(7, "S")
+        x_quant(1, 3)
+        w_regroup(0, 1, "G")
+        w_regroup(1, 1, "S")
+        store_linear(3)
+        store_linear(0)
         mm(0, 3)
+        t1(0, 0)
         t1(0, 1)
-        mm(0, 4)
+        mm(1, 0)
         t2(0, 0)
+        mm(1, 1)
+        t2(0, 1)
+        sin(0, 0)
+        w_quant(1, 1)
+        linear(1, "G")
+        sin(0, 1)
+        tr(0, 0)
+        t1(0, 2)
+        tr(0, 1)
+        t1(0, 3)
+        linear(2, "G")
+        mm(1, 2)
+        store_linear(1)
+        t2(0, 2)
+        mm(1, 3)
+        t2(0, 3)
+        sin(0, 2)
+        linear(4, "G")
+        store_linear(2)
+        w_quant(0, 1)
+        sin(0, 3)
+        tr(0, 2)
+        t1(1, 0)
+        outc(0, 0, "S")
+        tr(0, 3)
         linear(5, "G")
         store_linear(4)
-        t1(0, 2)
-        sin(0, 0)
-        t2(0, 1)
-        linear(6, "G")
-        tr(0, 0)
-        store_linear(5)
-        x_quant(0, 2)
-        sin(0, 1)
-        mm(0, 5)
-        t1(0, 3)
-        outc(0, 0, "S")
-        tr(0, 1)
-        linear(7, "G")
-        t2(0, 2)
-        store_linear(6)
-        mm(0, 6)
-        x_quant(1, 2)
-        sin(0, 2)
-        t1(0, 4)
-        outc(0, 1, "S")
-        store_linear(7)
-        tr(0, 2)
-        t2(0, 3)
-        mm(0, 7)
-        store(0, 0, 2)
-        x_quant(0, 3)
-        sin(0, 3)
-        t1(0, 5)
-        outc(0, 2, "S")
-        tr(0, 3)
-        t2(0, 4)
-        x_quant(1, 3)
-        sin(0, 4)
-        t1(0, 6)
-        mm(1, 0)
-        outc(0, 3, "S")
-        t2(0, 5)
-        tr(0, 4)
-        store(0, 2, 4)
-        t1(0, 7)
-        mm(1, 1)
-        sin(0, 5)
-        t2(0, 6)
-        outc(0, 4, "S")
-        tr(0, 5)
-        t1(1, 0)
-        sin(0, 6)
-        mm(1, 2)
-        t2(0, 7)
-        outc(0, 5, "S")
-        tr(0, 6)
         t1(1, 1)
-        sin(0, 7)
-        mm(1, 3)
-        store(0, 4, 6)
+        outc(0, 1, "S")
+        mm(0, 4)
         t2(1, 0)
-        outc(0, 6, "S")
-        tr(0, 7)
-        t1(1, 2)
-        sin(1, 0)
-        mm(1, 4)
+        store(0, 0, 2)
+        mm(0, 5)
+        linear(6, "G")
+        store_linear(5)
         t2(1, 1)
-        outc(0, 7, "S")
-        tr(1, 0)
-        t1(1, 3)
+        sin(1, 0)
+        t1(1, 2)
         sin(1, 1)
-        mm(1, 5)
-        store(0, 6, 8)
-        t2(1, 2)
-        outc(1, 0, "S")
+        tr(1, 0)
+        linear(7, "G")
+        store_linear(6)
+        t1(1, 3)
+        outc(0, 2, "S")
         tr(1, 1)
-        t1(1, 4)
-        sin(1, 2)
-        mm(1, 6)
+        t2(1, 2)
+        outc(0, 3, "S")
+        mm(0, 6)
         t2(1, 3)
-        outc(1, 1, "S")
-        tr(1, 2)
-        t1(1, 5)
+        store_linear(7)
+        sin(1, 2)
+        store(0, 2, 4)
+        mm(0, 7)
+        t1(0, 4)
         sin(1, 3)
-        mm(1, 7)
-        store(1, 0, 2)
-        t2(1, 4)
-        outc(1, 2, "S")
+        tr(1, 2)
+        t1(0, 5)
+        outc(1, 0, "S")
         tr(1, 3)
-        t1(1, 6)
-        sin(1, 4)
-        t2(1, 5)
+        t2(0, 4)
+        outc(1, 1, "S")
+        mm(1, 4)
+        t2(0, 5)
+        sin(0, 4)
+        store(1, 0, 2)
+        mm(1, 5)
+        t1(0, 6)
+        sin(0, 5)
+        tr(0, 4)
+        t1(0, 7)
+        outc(1, 2, "S")
+        tr(0, 5)
+        t2(0, 6)
         outc(1, 3, "S")
+        mm(1, 6)
+        t2(0, 7)
+        sin(0, 6)
+        store(1, 2, 4)
+        mm(1, 7)
+        t1(1, 4)
+        sin(0, 7)
+        tr(0, 6)
+        t1(1, 5)
+        outc(0, 4, "S")
+        tr(0, 7)
+        t2(1, 4)
+        outc(0, 5, "S")
+        t2(1, 5)
+        sin(1, 4)
+        store(0, 4, 6)
+        t1(1, 6)
+        sin(1, 5)
         tr(1, 4)
         t1(1, 7)
-        sin(1, 5)
-        store(1, 2, 4)
-        t2(1, 6)
-        outc(1, 4, "S")
+        outc(0, 6, "S")
         tr(1, 5)
+        t2(1, 6)
+        outc(0, 7, "S")
         t2(1, 7)
         sin(1, 6)
-        outc(1, 5, "S")
-        tr(1, 6)
+        store(0, 6, 8)
+        outc(1, 4, "V")
         sin(1, 7)
-        store(1, 4, 6)
-        outc(1, 6, "S")
+        tr(1, 6)
+        outc(1, 5, "V")
         tr(1, 7)
-        store(1, 6, 7)
-        outc(1, 7, "S")
-        store(1, 7, 8)
+        outc(1, 6, "S")
+        store(1, 4, 6)
+        outc(1, 7, "V")
+        store(1, 6, 8)

@@ -34,7 +34,7 @@ def tile_time2vec_kernel(tc, x, W, P, w, p, sine_w, cosine_w, out):
         keep = ctx.enter_context(tc.tile_pool(name="keep", bufs=1))
         small = ctx.enter_context(tc.tile_pool(name="small", bufs=1))
         linp = ctx.enter_context(tc.tile_pool(name="linp", bufs=8))
-        epi = ctx.enter_context(tc.tile_pool(name="epi", bufs=4))
+        epi = ctx.enter_context(tc.tile_pool(name="epi", bufs=6))
         psum = ctx.enter_context(tc.psum_pool(name="psum", bufs=8))
 
         x_view = x.rearrange("(p t) k -> p t k", t=NT)
@@ -61,7 +61,7 @@ def tile_time2vec_kernel(tc, x, W, P, w, p, sine_w, cosine_w, out):
         cs1 = small.tile([NP, 2], F32)
         c1 = cs1[:, 0:1]
         s1 = cs1[:, 1:2]
-        absc = col("absc")
+        ab = small.tile([NP, 2], F32)
         den = col("den")
         rden = col("rden")
         ang = small.tile([NP, 2], F32)
@@ -72,15 +72,16 @@ def tile_time2vec_kernel(tc, x, W, P, w, p, sine_w, cosine_w, out):
         rdd = col("rdd")
         tau = col("tau")
         tau2 = col("tau2")
-        h1 = col("h1")
-        h2 = col("h2")
-        h3 = col("h3")
+        ca = col("ca")
+        cb = col("cb")
+        t4 = col("t4")
+        ga = col("ga")
+        gb = col("gb")
+        hh = col("hh")
+        gg = col("gg")
         phi = col("phi")
         beta = small.tile([NP, NJ], F32)
         bturn = small.tile([NP, NJ], F32)
-        g1 = col("g1")
-        g2 = col("g2")
-        g3 = col("g3")
         dsg = col("dsg")
         amp = col("amp")
         xg = keep.tile([NP, NG, NT, 512], BF16, align_bytes=64)
@@ -238,165 +239,166 @@ def tile_time2vec_kernel(tc, x, W, P, w, p, sine_w, cosine_w, out):
         load_w1(0)
         load_w1(1)
         nc.gpsimd.tensor_copy(out=identb[:], in_=ident[:])
-        nc.vector.tensor_scalar(out=sc32[:], in0=raw16[:, :, 0], scalar1=GUARD, scalar2=None, op0=ALU.add)
+        nc.vector.tensor_scalar(out=sg2[:], in0=raw16[:, 3, 0:1], scalar1=0.0, scalar2=2.0, op0=ALU.is_ge, op1=ALU.mult)
+        nc.vector.scalar_tensor_tensor(out=ab[:], in0=raw16[:, 2:4, 0], scalar=-1.0, in1=raw16[:, 2:4, 0], op0=ALU.mult, op1=ALU.max)
+        nc.vector.tensor_copy(out=sc32[:], in_=raw16[:, :, 0])
         nc.tensor.transpose(out=pt[:], in_=prow[:], identity=identb[:])
-        nc.vector.tensor_scalar(out=sg2[:], in0=sc32[:, 3:4], scalar1=0.0, scalar2=2.0, op0=ALU.is_ge, op1=ALU.mult)
-        nc.vector.scalar_tensor_tensor(out=cs1[:], in0=sc32[:, 2:4], scalar=sg2[:], in1=sc32[:, 2:4], op0=ALU.mult, op1=ALU.subtract)
-        nc.vector.scalar_tensor_tensor(out=absc[:], in0=c1, scalar=-1.0, in1=c1, op0=ALU.mult, op1=ALU.max)
-        w_regroup(0, 0, "V")
-        nc.vector.tensor_scalar(out=den[:], in0=absc[:], scalar1=s1, scalar2=None, op0=ALU.add)
-        x_transpose(0)
+        nc.vector.scalar_tensor_tensor(out=cs1[:], in0=raw16[:, 2:4, 0], scalar=sg2[:], in1=raw16[:, 2:4, 0], op0=ALU.mult, op1=ALU.subtract)
+        nc.vector.tensor_scalar(out=den[:], in0=ab[:, 0:1], scalar1=ab[:, 1:2], scalar2=GUARD, op0=ALU.add, op1=ALU.add)
         nc.vector.reciprocal(out=rden[:], in_=den[:])
-        w_quant(0, 0)
-        x_transpose(1)
-        x_copy(0, "S")
         nc.vector.tensor_scalar(out=ang[:, 0:1], in0=c1, scalar1=rden[:], scalar2=0.5 * math.pi, op0=ALU.mult, op1=ALU.mult)
         nc.vector.tensor_scalar(out=ang[:, 1:2], in0=ang[:, 0:1], scalar1=0.5 * math.pi, scalar2=PI_BELOW, op0=ALU.add, op1=ALU.min)
-        x_copy(1, "S")
-        w_regroup(1, 0, "V")
+        w_regroup(0, 0, "V")
         nc.scalar.activation(out=sico[:], in_=ang[:], func=ACT.Sin)
-        nc.vector.tensor_scalar(out=tsin[:], in0=cs1[:], scalar1=sico[:, 0:1], scalar2=None, op0=ALU.mult)
-        x_transpose(2)
+        x_transpose(0)
+        nc.vector.tensor_scalar(out=tsin[:], in0=cs1[:], scalar1=sico[:, 0:1], scalar2=GUARD, op0=ALU.mult, op1=ALU.add)
+        x_transpose(1)
+        w_quant(0, 0)
+        x_copy(0, "S")
         nc.vector.scalar_tensor_tensor(out=dd[:], in0=s1, scalar=sico[:, 1:2], in1=tsin[:, 0:1], op0=ALU.mult, op1=ALU.add)
+        x_copy(1, "S")
         nc.vector.scalar_tensor_tensor(out=nn[:], in0=c1, scalar=sico[:, 1:2], in1=tsin[:, 1:2], op0=ALU.mult, op1=ALU.subtract)
+        w_regroup(1, 0, "V")
+        nc.vector.reciprocal(out=rdd[:], in_=dd[:])
+        x_transpose(2)
+        nc.vector.scalar_tensor_tensor(out=dsg[:], in0=dd[:], scalar=sg2[:], in1=dd[:], op0=ALU.mult, op1=ALU.subtract)
         x_quant(0, 0)
         x_transpose(3)
-        x_copy(2, "S")
-        nc.vector.reciprocal(out=rdd[:], in_=dd[:])
         nc.vector.tensor_scalar(out=tau[:], in0=nn[:], scalar1=rdd[:], scalar2=None, op0=ALU.mult)
         w_quant(1, 0)
-        x_copy(3, "S")
-        x_transpose(4)
+        x_copy(2, "S")
         nc.vector.tensor_scalar(out=tau2[:], in0=tau[:], scalar1=tau[:], scalar2=None, op0=ALU.mult)
-        x_transpose(5)
-        x_copy(4, "S")
-        nc.vector.tensor_scalar(out=h1[:], in0=tau2[:], scalar1=-1.0 / 7.0, scalar2=0.2, op0=ALU.mult, op1=ALU.add)
+        x_copy(3, "S")
         x_quant(1, 0)
-        nc.vector.tensor_scalar(out=h2[:], in0=h1[:], scalar1=tau2[:], scalar2=-1.0 / 3.0, op0=ALU.mult, op1=ALU.add)
-        x_copy(5, "S")
-        x_transpose(6)
-        nc.vector.tensor_scalar(out=h3[:], in0=h2[:], scalar1=tau2[:], scalar2=1.0, op0=ALU.mult, op1=ALU.add)
+        x_transpose(4)
+        nc.vector.tensor_scalar(out=ca[:], in0=tau2[:], scalar1=-1.0 / 3.0, scalar2=1.0, op0=ALU.mult, op1=ALU.add)
+        nc.vector.tensor_scalar(out=cb[:], in0=tau2[:], scalar1=-1.0 / 7.0, scalar2=0.2, op0=ALU.mult, op1=ALU.add)
+        x_transpose(5)
+        nc.vector.tensor_scalar(out=t4[:], in0=tau2[:], scalar1=tau2[:], scalar2=None, op0=ALU.mult)
+        nc.vector.tensor_scalar(out=ga[:], in0=tau2[:], scalar1=0.5, scalar2=1.0, op0=ALU.mult, op1=ALU.add)
+        x_copy(4, "S")
+        nc.vector.tensor_scalar(out=gb[:], in0=tau2[:], scalar1=1.0 / 16.0, scalar2=-0.125, op0=ALU.mult, op1=ALU.add)
         x_quant(0, 1)
-        x_transpose(7)
-        nc.vector.tensor_scalar(out=phi[:], in0=h3[:], scalar1=tau[:], scalar2=ang[:, 0:1], op0=ALU.mult, op1=ALU.add)
+        nc.vector.tensor_scalar(out=hh[:], in0=cb[:], scalar1=t4[:], scalar2=ca[:], op0=ALU.mult, op1=ALU.add)
+        nc.vector.tensor_scalar(out=gg[:], in0=gb[:], scalar1=t4[:], scalar2=ga[:], op0=ALU.mult, op1=ALU.add)
+        x_copy(5, "S")
         x_quant(1, 1)
+        x_transpose(6)
+        nc.vector.tensor_scalar(out=phi[:], in0=hh[:], scalar1=tau[:], scalar2=ang[:, 0:1], op0=ALU.mult, op1=ALU.add)
+        nc.vector.tensor_scalar(out=amp[:], in0=gg[:], scalar1=dsg[:], scalar2=None, op0=ALU.mult)
+        x_transpose(7)
         x_copy(6, "S")
+        x_quant(0, 2)
+        mm(0, 0)
         nc.vector.tensor_scalar(out=beta[:], in0=pt[:, 0:NJ], scalar1=phi[:], scalar2=None, op0=ALU.add)
         nc.vector.tensor_scalar(out=bturn[:], in0=pt[:, 0:NJ], scalar1=phi[:], scalar2=TURN, op0=ALU.add, op1=ALU.mult)
-        mm(0, 0)
-        x_quant(0, 2)
-        x_copy(7, "S")
         nc.vector.tensor_copy(out=sc32g[:], in_=sc32[:, 0:2])
-        nc.vector.tensor_scalar(out=g1[:], in0=tau2[:], scalar1=1.0 / 16.0, scalar2=-0.125, op0=ALU.mult, op1=ALU.add)
+        x_copy(7, "S")
         x_quant(1, 2)
-        linear(3, "G")
+        linear(0, "G")
         mm(0, 1)
-        linear(0, "S")
-        nc.vector.tensor_scalar(out=g2[:], in0=g1[:], scalar1=tau2[:], scalar2=0.5, op0=ALU.mult, op1=ALU.add)
-        nc.vector.tensor_scalar(out=g3[:], in0=g2[:], scalar1=tau2[:], scalar2=1.0, op0=ALU.mult, op1=ALU.add)
         x_quant(0, 3)
-        mm(0, 2)
-        nc.vector.scalar_tensor_tensor(out=dsg[:], in0=dd[:], scalar=sg2[:], in1=dd[:], op0=ALU.mult, op1=ALU.subtract)
-        nc.vector.tensor_scalar(out=amp[:], in0=g3[:], scalar1=dsg[:], scalar2=None, op0=ALU.mult)
         x_quant(1, 3)
-        w_regroup(0, 1, "G")
-        w_regroup(1, 1, "S")
-        store_linear(3)
-        store_linear(0)
-        mm(0, 3)
+        mm(0, 2)
         t1(0, 0)
+        linear(1, "G")
+        store_linear(0)
+        w_regroup(1, 1, "S")
+        mm(0, 3)
         t1(0, 1)
         mm(1, 0)
         t2(0, 0)
+        linear(2, "G")
+        store_linear(1)
         mm(1, 1)
         t2(0, 1)
-        sin(0, 0)
+        w_regroup(0, 1, "S")
+        linear(3, "G")
         w_quant(1, 1)
-        linear(1, "G")
-        sin(0, 1)
-        tr(0, 0)
-        t1(0, 2)
-        tr(0, 1)
-        t1(0, 3)
-        linear(2, "G")
-        mm(1, 2)
-        store_linear(1)
-        t2(0, 2)
-        mm(1, 3)
-        t2(0, 3)
-        sin(0, 2)
-        linear(4, "G")
         store_linear(2)
-        w_quant(0, 1)
-        sin(0, 3)
-        tr(0, 2)
-        t1(1, 0)
-        outc(0, 0, "S")
-        tr(0, 3)
+        t1(0, 2)
+        linear(4, "G")
+        t1(0, 3)
+        store_linear(3)
+        t2(0, 2)
+        sin(0, 0)
+        t2(0, 3)
         linear(5, "G")
         store_linear(4)
-        t1(1, 1)
-        outc(0, 1, "S")
-        mm(0, 4)
-        t2(1, 0)
-        store(0, 0, 2)
-        mm(0, 5)
+        sin(0, 1)
+        tr(0, 0)
+        w_quant(0, 1)
+        sin(0, 2)
+        tr(0, 1)
+        t1(1, 0)
         linear(6, "G")
         store_linear(5)
-        t2(1, 1)
-        sin(1, 0)
-        t1(1, 2)
-        sin(1, 1)
-        tr(1, 0)
+        sin(0, 3)
+        mm(1, 2)
+        t1(1, 1)
+        outc(0, 0, "S")
+        mm(1, 3)
+        t2(1, 0)
         linear(7, "G")
         store_linear(6)
+        outc(0, 1, "S")
+        tr(0, 2)
+        t2(1, 1)
+        sin(1, 0)
+        tr(0, 3)
+        store(0, 0, 2)
+        t1(1, 2)
+        sin(1, 1)
+        mm(0, 4)
+        store_linear(7)
         t1(1, 3)
         outc(0, 2, "S")
-        tr(1, 1)
+        mm(0, 5)
         t2(1, 2)
         outc(0, 3, "S")
-        mm(0, 6)
+        tr(1, 0)
         t2(1, 3)
-        store_linear(7)
         sin(1, 2)
+        tr(1, 1)
         store(0, 2, 4)
-        mm(0, 7)
         t1(0, 4)
+        mm(0, 6)
         sin(1, 3)
-        tr(1, 2)
         t1(0, 5)
         outc(1, 0, "S")
-        tr(1, 3)
+        mm(0, 7)
         t2(0, 4)
         outc(1, 1, "S")
-        mm(1, 4)
+        tr(1, 2)
         t2(0, 5)
         sin(0, 4)
+        tr(1, 3)
         store(1, 0, 2)
-        mm(1, 5)
         t1(0, 6)
+        mm(1, 4)
         sin(0, 5)
-        tr(0, 4)
         t1(0, 7)
         outc(1, 2, "S")
-        tr(0, 5)
+        mm(1, 5)
         t2(0, 6)
         outc(1, 3, "S")
-        mm(1, 6)
+        tr(0, 4)
         t2(0, 7)
         sin(0, 6)
+        tr(0, 5)
         store(1, 2, 4)
-        mm(1, 7)
         t1(1, 4)
+        mm(1, 6)
         sin(0, 7)
-        tr(0, 6)
         t1(1, 5)
         outc(0, 4, "S")
-        tr(0, 7)
+        mm(1, 7)
         t2(1, 4)
         outc(0, 5, "S")
+        tr(0, 6)
         t2(1, 5)
         sin(1, 4)
+        tr(0, 7)
         store(0, 4, 6)
         t1(1, 6)
         sin(1, 5)

@@ -51,8 +51,9 @@ def tile_time2vec_kernel(tc, x, W, P, w, p, sine_w, cosine_w, out):
         junk = small.tile([NP, 1], F32)
         ident = keep.tile([NP, NP], F32)
         identb = keep.tile([NP, NP], BF16)
-        x_sb = keep.tile([NP, NT, K], BF16)
-        w_raw = keep.tile([NP, NG, 4, N], BF16)
+        x_sb = [keep.tile([NP, 2, K], BF16, name="x_sb%d" % j) for j in range(NT // 2)]
+        w_raw = [[keep.tile([NP, 4, 512], BF16, name="w_raw%d%d" % (g, h)) for h in range(1)] for g in range(NG)]
+        w_raw1 = keep.tile([NP, NG, 4, 512], BF16)
         sc32 = small.tile([NP, 4], F32)
         w32 = sc32[:, 0:1]
         p32 = sc32[:, 1:2]
@@ -84,13 +85,12 @@ def tile_time2vec_kernel(tc, x, W, P, w, p, sine_w, cosine_w, out):
         bturn = small.tile([NP, NJ], F32)
         dsg = col("dsg")
         amp = col("amp")
-        xg = keep.tile([NP, NG, NT, 512], BF16, align_bytes=64)
+        xg = [keep.tile([NP, NG, 512], BF16, name="xg%d" % t, align_bytes=64) for t in range(NT)]
         xc = keep.tile([NP, NG, B], U32, align_bytes=64)
         xs = keep.tile([NP, NG, B], U8, align_bytes=64)
-        wg = keep.tile([NP, NG, N, 4], BF16, align_bytes=64)
+        wg = [[keep.tile([NP, 512, 4], BF16, name="wg%d%d" % (g, h), align_bytes=64) for h in range(2)] for g in range(NG)]
         wc = keep.tile([NP, NG, N], U32, align_bytes=64)
         ws = keep.tile([NP, NG, N], U8, align_bytes=64)
-        stages = [keep.tile([NP, 4, N], F32, name="stage%d" % hb) for hb in range(NHB)]
         live = {}
         scalars = (w, p, cosine_w, sine_w)
 
@@ -98,69 +98,67 @@ def tile_time2vec_kernel(tc, x, W, P, w, p, sine_w, cosine_w, out):
             with nc.allow_non_contiguous_dma(reason="one element a partition"):
                 nc.scalar.dma_start(out=raw16[:, j, 0:1], in_=scalars[j].partition_broadcast(NP))
 
+        def load_p():
+            nc.scalar.dma_start(out=prow[0:NJ, :], in_=P.rearrange("(j n) -> j n", n=NP))
+
         def load_x(j):
-            nc.sync.dma_start(out=x_sb[:, 2 * j : 2 * j + 2, :], in_=x_view[:, 2 * j : 2 * j + 2, :])
+            nc.sync.dma_start(out=x_sb[j][:], in_=x_view[:, 2 * j : 2 * j + 2, :])
 
         def load_w0(g, u):
-            nc.sync.dma_start(out=w_raw[:, g, 2 * u : 2 * u + 2, 0:512], in_=w_view0[g, u][:, :, 0:512])
+            nc.sync.dma_start(out=w_raw[g][0][:, 2 * u : 2 * u + 2, :], in_=w_view0[g, u][:, :, 0:512])
 
         def load_w1(e):
             nc.sync.dma_start(
-                out=w_raw[:].rearrange("p g (u e) c -> p (g u) e c", e=2)[:, :, e, 512:N], in_=w_view1[e][:, :, 512:N]
+                out=w_raw1[:].rearrange("p g (u e) c -> p (g u) e c", e=2)[:, :, e, :], in_=w_view1[e][:, :, 512:N]
             )
 
         def x_transpose(t):
             xt = psum.tile([NP, 4, NP], F32, tag="bank", name="xt%d" % t)
-            xw = x_sb[:, t, :].bitcast(F32)
+            xw = x_sb[t // 2][:, t % 2, :].bitcast(F32)
             for j in range(4):
                 nc.tensor.transpose(out=xt[:, j, :], in_=xw[:, NP * j : NP * j + NP], identity=ident[:])
             live[("xt", t)] = xt
 
         def x_copy(t, eng):
-            dst = xg[:, :, t, :].bitcast(F32).rearrange("p g (b u) -> p g b u", u=2)
+            dst = xg[t][:].bitcast(F32).rearrange("p g (b u) -> p g b u", u=2)
             src = live[("xt", t)][:].rearrange("p (g u) b -> p g b u", g=NG, u=2)
             if eng == "S":
                 nc.scalar.copy(out=dst, in_=src)
             else:
                 nc.vector.tensor_copy(out=dst, in_=src)
 
-        def x_quant(g, jj):
+        def x_quant(g, t):
             nc.vector.quantize_mx(
-                out=xc[:, g, 256 * jj : 256 * jj + 256].bitcast(FP8X4),
-                scales=xs[:, g, 256 * jj : 256 * jj + 256],
-                in_=xg[:, g, 2 * jj : 2 * jj + 2, :].rearrange("p t c -> p (t c)"),
+                out=xc[:, g, NP * t : NP * t + NP].bitcast(FP8X4), scales=xs[:, g, NP * t : NP * t + NP], in_=xg[t][:, g, :]
             )
 
         def linear(t, eng):
             lin = linp.tile([NP, K], F32, name="lin")
+            src = x_sb[t // 2][:, t % 2, :]
             if eng == "S":
-                nc.scalar.activation(out=lin[:], in_=x_sb[:, t, :], func=ACT.Identity, scale=w32, bias=p32)
+                nc.scalar.activation(out=lin[:], in_=src, func=ACT.Identity, scale=w32, bias=p32)
             elif eng == "G":
-                nc.gpsimd.tensor_scalar(out=lin[:], in0=x_sb[:, t, :], scalar1=sc32g[:, 0:1], scalar2=sc32g[:, 1:2], op0=ALU.mult, op1=ALU.add)
+                nc.gpsimd.tensor_scalar(out=lin[:], in0=src, scalar1=sc32g[:, 0:1], scalar2=sc32g[:, 1:2], op0=ALU.mult, op1=ALU.add)
             else:
-                nc.vector.tensor_scalar(out=lin[:], in0=x_sb[:, t, :], scalar1=w32, scalar2=p32, op0=ALU.mult, op1=ALU.add)
+                nc.vector.tensor_scalar(out=lin[:], in0=src, scalar1=w32, scalar2=p32, op0=ALU.mult, op1=ALU.add)
             live[("lin", t)] = lin
 
         def store_linear(t):
             nc.sync.dma_start(out=out_view[:, t, 0:K], in_=live[("lin", t)][:])
 
         def w_regroup(g, h, eng):
-            cols = slice(512 * h, 512 * h + 512)
-            dst = wg[:, g, cols, :].rearrange("p (c i) t -> p c t i", i=4)
-            src = w_raw[:, g, :, cols].rearrange("p t (c i) -> p c t i", i=4)
+            dst = wg[g][h][:].rearrange("p (c i) t -> p c t i", i=4)
+            raw = w_raw[g][0][:] if h == 0 else w_raw1[:, g]
+            src = raw.rearrange("p t (c i) -> p c t i", i=4)
             if eng == "S":
                 nc.scalar.copy(out=dst, in_=src)
-            elif eng == "G":
-                nc.gpsimd.tensor_scalar(out=dst, in0=src, scalar1=1.0, scalar2=0.0, op0=ALU.mult, op1=ALU.add)
             else:
                 nc.vector.tensor_copy(out=dst, in_=src)
 
         def w_quant(g, h):
             cols = slice(512 * h, 512 * h + 512)
             nc.vector.quantize_mx(
-                out=wc[:, g, cols].bitcast(FP8X4),
-                scales=ws[:, g, cols],
-                in_=wg[:, g, cols, :].rearrange("p c t -> p (c t)"),
+                out=wc[:, g, cols].bitcast(FP8X4), scales=ws[:, g, cols], in_=wg[g][h][:].rearrange("p c t -> p (c t)")
             )
 
         def mm(hb, j):
@@ -205,17 +203,20 @@ def tile_time2vec_kernel(tc, x, W, P, w, p, sine_w, cosine_w, out):
                 nc.tensor.transpose(out=ob[:, i, :], in_=sn[:, NP * i : NP * i + NP], identity=ident[:])
             live[("o", hb, j)] = ob
 
+        groups = [[[0,2],[2,4],[4,6],[6,8]],[[0,2],[2,4],[4,6],[6,8]]]
+
         def outc(hb, j, eng):
-            dst = stages[hb][:, :, NP * j : NP * j + NP]
+            j0, j1 = [gr for gr in groups[hb] if gr[0] <= j < gr[1]][0]
+            if ("st", hb, j0) not in live:
+                live[("st", hb, j0)] = keep.tile([NP, 4, NP * (j1 - j0)], F32, name="stage%d%d" % (hb, j0))
+            dst = live[("st", hb, j0)][:, :, NP * (j - j0) : NP * (j - j0) + NP]
             if eng == "S":
                 nc.scalar.activation(out=dst, in_=live[("o", hb, j)][:], func=ACT.Copy, scale=amp[:])
             else:
                 nc.vector.tensor_scalar(out=dst, in0=live[("o", hb, j)][:], scalar1=amp[:], scalar2=None, op0=ALU.mult)
 
         def store(hb, j0, j1):
-            nc.sync.dma_start(
-                out=out_view[:, 4 * hb : 4 * hb + 4, K + NP * j0 : K + NP * j1], in_=stages[hb][:, :, NP * j0 : NP * j1]
-            )
+            nc.sync.dma_start(out=out_view[:, 4 * hb : 4 * hb + 4, K + NP * j0 : K + NP * j1], in_=live[("st", hb, j0)][:])
 
         ctx.enter_context(tc.manual_schedule())
         nc.vector.memset(prow[:], 0.0)
@@ -230,7 +231,7 @@ def tile_time2vec_kernel(tc, x, W, P, w, p, sine_w, cosine_w, out):
         load_x(0)
         load_scalar(3)
         load_w0(1, 0)
-        nc.scalar.dma_start(out=prow[0:NJ, :], in_=P.rearrange("(j n) -> j n", n=NP))
+        load_p()
         load_w0(1, 1)
         nc.scalar.activation(out=junk[:], in_=warm[:], func=ACT.Sin)
         load_x(1)
@@ -263,67 +264,75 @@ def tile_time2vec_kernel(tc, x, W, P, w, p, sine_w, cosine_w, out):
         x_transpose(2)
         nc.vector.scalar_tensor_tensor(out=dsg[:], in0=dd[:], scalar=sg2[:], in1=dd[:], op0=ALU.mult, op1=ALU.subtract)
         x_quant(0, 0)
+        x_quant(1, 0)
         x_transpose(3)
         nc.vector.tensor_scalar(out=tau[:], in0=nn[:], scalar1=rdd[:], scalar2=None, op0=ALU.mult)
         w_quant(1, 0)
         x_copy(2, "S")
-        nc.vector.tensor_scalar(out=tau2[:], in0=tau[:], scalar1=tau[:], scalar2=None, op0=ALU.mult)
         x_copy(3, "S")
-        x_quant(1, 0)
-        x_transpose(4)
-        nc.vector.tensor_scalar(out=ca[:], in0=tau2[:], scalar1=-1.0 / 3.0, scalar2=1.0, op0=ALU.mult, op1=ALU.add)
-        nc.vector.tensor_scalar(out=cb[:], in0=tau2[:], scalar1=-1.0 / 7.0, scalar2=0.2, op0=ALU.mult, op1=ALU.add)
-        x_transpose(5)
-        nc.vector.tensor_scalar(out=t4[:], in0=tau2[:], scalar1=tau2[:], scalar2=None, op0=ALU.mult)
-        nc.vector.tensor_scalar(out=ga[:], in0=tau2[:], scalar1=0.5, scalar2=1.0, op0=ALU.mult, op1=ALU.add)
-        x_copy(4, "S")
-        nc.vector.tensor_scalar(out=gb[:], in0=tau2[:], scalar1=1.0 / 16.0, scalar2=-0.125, op0=ALU.mult, op1=ALU.add)
+        nc.vector.tensor_scalar(out=tau2[:], in0=tau[:], scalar1=tau[:], scalar2=None, op0=ALU.mult)
         x_quant(0, 1)
-        nc.vector.tensor_scalar(out=hh[:], in0=cb[:], scalar1=t4[:], scalar2=ca[:], op0=ALU.mult, op1=ALU.add)
-        nc.vector.tensor_scalar(out=gg[:], in0=gb[:], scalar1=t4[:], scalar2=ga[:], op0=ALU.mult, op1=ALU.add)
-        x_copy(5, "S")
+        x_transpose(4)
         x_quant(1, 1)
-        x_transpose(6)
-        nc.vector.tensor_scalar(out=phi[:], in0=hh[:], scalar1=tau[:], scalar2=ang[:, 0:1], op0=ALU.mult, op1=ALU.add)
-        nc.vector.tensor_scalar(out=amp[:], in0=gg[:], scalar1=dsg[:], scalar2=None, op0=ALU.mult)
-        x_transpose(7)
-        x_copy(6, "S")
+        nc.vector.tensor_scalar(out=ca[:], in0=tau2[:], scalar1=-1.0 / 3.0, scalar2=1.0, op0=ALU.mult, op1=ALU.add)
+        x_transpose(5)
+        nc.vector.tensor_scalar(out=cb[:], in0=tau2[:], scalar1=-1.0 / 7.0, scalar2=0.2, op0=ALU.mult, op1=ALU.add)
+        nc.vector.tensor_scalar(out=t4[:], in0=tau2[:], scalar1=tau2[:], scalar2=None, op0=ALU.mult)
+        x_copy(4, "S")
+        nc.vector.tensor_scalar(out=ga[:], in0=tau2[:], scalar1=0.5, scalar2=1.0, op0=ALU.mult, op1=ALU.add)
+        nc.vector.tensor_scalar(out=gb[:], in0=tau2[:], scalar1=1.0 / 16.0, scalar2=-0.125, op0=ALU.mult, op1=ALU.add)
         x_quant(0, 2)
+        x_quant(1, 2)
+        nc.vector.tensor_scalar(out=hh[:], in0=cb[:], scalar1=t4[:], scalar2=ca[:], op0=ALU.mult, op1=ALU.add)
+        x_copy(5, "S")
+        nc.vector.tensor_scalar(out=gg[:], in0=gb[:], scalar1=t4[:], scalar2=ga[:], op0=ALU.mult, op1=ALU.add)
+        x_transpose(6)
+        x_quant(0, 3)
+        x_quant(1, 3)
+        nc.vector.tensor_scalar(out=phi[:], in0=hh[:], scalar1=tau[:], scalar2=ang[:, 0:1], op0=ALU.mult, op1=ALU.add)
+        x_transpose(7)
+        nc.vector.tensor_scalar(out=amp[:], in0=gg[:], scalar1=dsg[:], scalar2=None, op0=ALU.mult)
+        x_quant(0, 4)
+        x_copy(6, "S")
+        x_quant(1, 4)
         mm(0, 0)
         nc.vector.tensor_scalar(out=beta[:], in0=pt[:, 0:NJ], scalar1=phi[:], scalar2=None, op0=ALU.add)
         nc.vector.tensor_scalar(out=bturn[:], in0=pt[:, 0:NJ], scalar1=phi[:], scalar2=TURN, op0=ALU.add, op1=ALU.mult)
         nc.vector.tensor_copy(out=sc32g[:], in_=sc32[:, 0:2])
         x_copy(7, "S")
-        x_quant(1, 2)
+        x_quant(0, 5)
         linear(0, "G")
+        x_quant(1, 5)
+        x_quant(0, 6)
         mm(0, 1)
-        x_quant(0, 3)
-        x_quant(1, 3)
-        mm(0, 2)
+        x_quant(1, 6)
+        x_quant(0, 7)
+        x_quant(1, 7)
         t1(0, 0)
+        mm(0, 2)
         linear(1, "G")
         store_linear(0)
+        t1(0, 1)
         w_regroup(1, 1, "S")
         mm(0, 3)
-        t1(0, 1)
-        mm(1, 0)
         t2(0, 0)
+        mm(1, 0)
         linear(2, "G")
         store_linear(1)
-        mm(1, 1)
         t2(0, 1)
-        w_regroup(0, 1, "S")
+        mm(1, 1)
         linear(3, "G")
-        w_quant(1, 1)
+        w_regroup(0, 1, "S")
         store_linear(2)
+        w_quant(1, 1)
         t1(0, 2)
         linear(4, "G")
         t1(0, 3)
         store_linear(3)
         t2(0, 2)
         sin(0, 0)
-        t2(0, 3)
         linear(5, "G")
+        t2(0, 3)
         store_linear(4)
         sin(0, 1)
         tr(0, 0)

@@ -45,7 +45,8 @@ def tile_time2vec_kernel(tc, x, W, P, w, p, sine_w, cosine_w, out):
         def col(name):
             return small.tile([NP, 1], F32, name=name)
 
-        raw16 = small.tile([NP, 4, 16], BF16)
+        srow = keep.tile([NP, 64], BF16)
+        ones = keep.tile([NP, NP], BF16)
         prow = keep.tile([NP, NP], BF16)
         warm = small.tile([NP, 1], F32)
         junk = small.tile([NP, 1], F32)
@@ -95,8 +96,7 @@ def tile_time2vec_kernel(tc, x, W, P, w, p, sine_w, cosine_w, out):
         scalars = (w, p, cosine_w, sine_w)
 
         def load_scalar(j):
-            with nc.allow_non_contiguous_dma(reason="one element a partition"):
-                nc.scalar.dma_start(out=raw16[:, j, 0:1], in_=scalars[j].partition_broadcast(NP))
+            nc.scalar.dma_start(out=srow[0:1, 16 * j : 16 * j + 1], in_=scalars[j].rearrange("(o n) -> o n", o=1))
 
         def load_p():
             nc.scalar.dma_start(out=prow[0:NJ, :], in_=P.rearrange("(j n) -> j n", n=NP))
@@ -221,6 +221,9 @@ def tile_time2vec_kernel(tc, x, W, P, w, p, sine_w, cosine_w, out):
         ctx.enter_context(tc.manual_schedule())
         nc.vector.memset(prow[:], 0.0)
         nc.vector.memset(warm[:], 0.0)
+        nc.vector.memset(srow[:], 0.0)
+        nc.vector.memset(ones[:], 1.0)
+        sp = psum.tile([NP, 4, 16], F32, tag="bank", name="sp")
         pt = psum.tile([NP, NP], BF16, tag="bank", name="pt")
         load_scalar(0)
         load_w0(0, 0)
@@ -240,130 +243,131 @@ def tile_time2vec_kernel(tc, x, W, P, w, p, sine_w, cosine_w, out):
         load_w1(0)
         load_w1(1)
         nc.gpsimd.tensor_copy(out=identb[:], in_=ident[:])
-        nc.vector.tensor_scalar(out=sg2[:], in0=raw16[:, 3, 0:1], scalar1=0.0, scalar2=2.0, op0=ALU.is_ge, op1=ALU.mult)
-        nc.vector.scalar_tensor_tensor(out=ab[:], in0=raw16[:, 2:4, 0], scalar=-1.0, in1=raw16[:, 2:4, 0], op0=ALU.mult, op1=ALU.max)
-        nc.vector.tensor_copy(out=sc32[:], in_=raw16[:, :, 0])
-        nc.tensor.transpose(out=pt[:], in_=prow[:], identity=identb[:])
-        nc.vector.scalar_tensor_tensor(out=cs1[:], in0=raw16[:, 2:4, 0], scalar=sg2[:], in1=raw16[:, 2:4, 0], op0=ALU.mult, op1=ALU.subtract)
-        nc.vector.tensor_scalar(out=den[:], in0=ab[:, 0:1], scalar1=ab[:, 1:2], scalar2=GUARD, op0=ALU.add, op1=ALU.add)
-        nc.vector.reciprocal(out=rden[:], in_=den[:])
-        nc.vector.tensor_scalar(out=ang[:, 0:1], in0=c1, scalar1=rden[:], scalar2=0.5 * math.pi, op0=ALU.mult, op1=ALU.mult)
-        nc.vector.tensor_scalar(out=ang[:, 1:2], in0=ang[:, 0:1], scalar1=0.5 * math.pi, scalar2=PI_BELOW, op0=ALU.add, op1=ALU.min)
+        nc.tensor.matmul(out=sp[:].rearrange("p j k -> p (j k)"), lhsT=ones[:], rhs=srow[:], start=True, stop=True)
         w_regroup(0, 0, "V")
-        nc.scalar.activation(out=sico[:], in_=ang[:], func=ACT.Sin)
+        nc.vector.tensor_copy(out=sc32[:], in_=sp[:, :, 0])
         x_transpose(0)
-        nc.vector.tensor_scalar(out=tsin[:], in0=cs1[:], scalar1=sico[:, 0:1], scalar2=GUARD, op0=ALU.mult, op1=ALU.add)
-        x_transpose(1)
+        nc.vector.tensor_scalar(out=sg2[:], in0=sc32[:, 3:4], scalar1=0.0, scalar2=2.0, op0=ALU.is_ge, op1=ALU.mult)
+        nc.vector.scalar_tensor_tensor(out=ab[:], in0=sc32[:, 2:4], scalar=-1.0, in1=sc32[:, 2:4], op0=ALU.mult, op1=ALU.max)
         w_quant(0, 0)
+        x_transpose(1)
         x_copy(0, "S")
-        nc.vector.scalar_tensor_tensor(out=dd[:], in0=s1, scalar=sico[:, 1:2], in1=tsin[:, 0:1], op0=ALU.mult, op1=ALU.add)
+        nc.vector.scalar_tensor_tensor(out=cs1[:], in0=sc32[:, 2:4], scalar=sg2[:], in1=sc32[:, 2:4], op0=ALU.mult, op1=ALU.subtract)
+        nc.vector.tensor_scalar(out=den[:], in0=ab[:, 0:1], scalar1=ab[:, 1:2], scalar2=GUARD, op0=ALU.add, op1=ALU.add)
         x_copy(1, "S")
-        nc.vector.scalar_tensor_tensor(out=nn[:], in0=c1, scalar=sico[:, 1:2], in1=tsin[:, 1:2], op0=ALU.mult, op1=ALU.subtract)
+        nc.vector.reciprocal(out=rden[:], in_=den[:])
         w_regroup(1, 0, "V")
-        nc.vector.reciprocal(out=rdd[:], in_=dd[:])
+        nc.vector.tensor_scalar(out=ang[:, 0:1], in0=c1, scalar1=rden[:], scalar2=0.5 * math.pi, op0=ALU.mult, op1=ALU.mult)
         x_transpose(2)
-        nc.vector.scalar_tensor_tensor(out=dsg[:], in0=dd[:], scalar=sg2[:], in1=dd[:], op0=ALU.mult, op1=ALU.subtract)
+        nc.vector.tensor_scalar(out=ang[:, 1:2], in0=ang[:, 0:1], scalar1=0.5 * math.pi, scalar2=PI_BELOW, op0=ALU.add, op1=ALU.min)
         x_quant(0, 0)
-        x_quant(1, 0)
+        nc.scalar.activation(out=sico[:], in_=ang[:], func=ACT.Sin)
         x_transpose(3)
-        nc.vector.tensor_scalar(out=tau[:], in0=nn[:], scalar1=rdd[:], scalar2=None, op0=ALU.mult)
-        w_quant(1, 0)
+        x_quant(1, 0)
         x_copy(2, "S")
+        w_quant(1, 0)
+        nc.tensor.transpose(out=pt[:], in_=prow[:], identity=identb[:])
         x_copy(3, "S")
-        nc.vector.tensor_scalar(out=tau2[:], in0=tau[:], scalar1=tau[:], scalar2=None, op0=ALU.mult)
-        x_quant(0, 1)
+        nc.vector.tensor_scalar(out=tsin[:], in0=cs1[:], scalar1=sico[:, 0:1], scalar2=GUARD, op0=ALU.mult, op1=ALU.add)
         x_transpose(4)
+        x_quant(0, 1)
         x_quant(1, 1)
-        nc.vector.tensor_scalar(out=ca[:], in0=tau2[:], scalar1=-1.0 / 3.0, scalar2=1.0, op0=ALU.mult, op1=ALU.add)
+        nc.vector.scalar_tensor_tensor(out=dd[:], in0=s1, scalar=sico[:, 1:2], in1=tsin[:, 0:1], op0=ALU.mult, op1=ALU.add)
         x_transpose(5)
-        nc.vector.tensor_scalar(out=cb[:], in0=tau2[:], scalar1=-1.0 / 7.0, scalar2=0.2, op0=ALU.mult, op1=ALU.add)
-        nc.vector.tensor_scalar(out=t4[:], in0=tau2[:], scalar1=tau2[:], scalar2=None, op0=ALU.mult)
+        nc.vector.scalar_tensor_tensor(out=nn[:], in0=c1, scalar=sico[:, 1:2], in1=tsin[:, 1:2], op0=ALU.mult, op1=ALU.subtract)
         x_copy(4, "S")
-        nc.vector.tensor_scalar(out=ga[:], in0=tau2[:], scalar1=0.5, scalar2=1.0, op0=ALU.mult, op1=ALU.add)
-        nc.vector.tensor_scalar(out=gb[:], in0=tau2[:], scalar1=1.0 / 16.0, scalar2=-0.125, op0=ALU.mult, op1=ALU.add)
         x_quant(0, 2)
         x_quant(1, 2)
-        nc.vector.tensor_scalar(out=hh[:], in0=cb[:], scalar1=t4[:], scalar2=ca[:], op0=ALU.mult, op1=ALU.add)
-        x_copy(5, "S")
-        nc.vector.tensor_scalar(out=gg[:], in0=gb[:], scalar1=t4[:], scalar2=ga[:], op0=ALU.mult, op1=ALU.add)
-        x_transpose(6)
+        nc.vector.reciprocal(out=rdd[:], in_=dd[:])
+        nc.vector.scalar_tensor_tensor(out=dsg[:], in0=dd[:], scalar=sg2[:], in1=dd[:], op0=ALU.mult, op1=ALU.subtract)
         x_quant(0, 3)
+        x_copy(5, "S")
         x_quant(1, 3)
-        nc.vector.tensor_scalar(out=phi[:], in0=hh[:], scalar1=tau[:], scalar2=ang[:, 0:1], op0=ALU.mult, op1=ALU.add)
-        x_transpose(7)
-        nc.vector.tensor_scalar(out=amp[:], in0=gg[:], scalar1=dsg[:], scalar2=None, op0=ALU.mult)
+        x_transpose(6)
+        nc.vector.tensor_scalar(out=tau[:], in0=nn[:], scalar1=rdd[:], scalar2=None, op0=ALU.mult)
         x_quant(0, 4)
-        x_copy(6, "S")
+        x_transpose(7)
+        nc.vector.tensor_scalar(out=tau2[:], in0=tau[:], scalar1=tau[:], scalar2=None, op0=ALU.mult)
         x_quant(1, 4)
+        x_copy(6, "S")
+        nc.vector.tensor_scalar(out=ca[:], in0=tau2[:], scalar1=-1.0 / 3.0, scalar2=1.0, op0=ALU.mult, op1=ALU.add)
+        nc.vector.tensor_scalar(out=cb[:], in0=tau2[:], scalar1=-1.0 / 7.0, scalar2=0.2, op0=ALU.mult, op1=ALU.add)
         mm(0, 0)
+        nc.vector.tensor_scalar(out=t4[:], in0=tau2[:], scalar1=tau2[:], scalar2=None, op0=ALU.mult)
+        nc.vector.tensor_scalar(out=ga[:], in0=tau2[:], scalar1=0.5, scalar2=1.0, op0=ALU.mult, op1=ALU.add)
+        nc.vector.tensor_scalar(out=gb[:], in0=tau2[:], scalar1=1.0 / 16.0, scalar2=-0.125, op0=ALU.mult, op1=ALU.add)
+        x_quant(0, 5)
+        x_copy(7, "S")
+        nc.vector.tensor_scalar(out=hh[:], in0=cb[:], scalar1=t4[:], scalar2=ca[:], op0=ALU.mult, op1=ALU.add)
+        nc.vector.tensor_scalar(out=gg[:], in0=gb[:], scalar1=t4[:], scalar2=ga[:], op0=ALU.mult, op1=ALU.add)
+        x_quant(1, 5)
+        mm(0, 1)
+        nc.vector.tensor_scalar(out=phi[:], in0=hh[:], scalar1=tau[:], scalar2=ang[:, 0:1], op0=ALU.mult, op1=ALU.add)
+        nc.vector.tensor_scalar(out=amp[:], in0=gg[:], scalar1=dsg[:], scalar2=None, op0=ALU.mult)
+        x_quant(0, 6)
         nc.vector.tensor_scalar(out=beta[:], in0=pt[:, 0:NJ], scalar1=phi[:], scalar2=None, op0=ALU.add)
         nc.vector.tensor_scalar(out=bturn[:], in0=pt[:, 0:NJ], scalar1=phi[:], scalar2=TURN, op0=ALU.add, op1=ALU.mult)
         nc.vector.tensor_copy(out=sc32g[:], in_=sc32[:, 0:2])
-        x_copy(7, "S")
-        x_quant(0, 5)
-        linear(0, "G")
-        x_quant(1, 5)
-        x_quant(0, 6)
-        mm(0, 1)
+        mm(0, 2)
         x_quant(1, 6)
+        linear(0, "G")
         x_quant(0, 7)
         x_quant(1, 7)
         t1(0, 0)
-        mm(0, 2)
-        linear(1, "G")
-        store_linear(0)
-        t1(0, 1)
         w_regroup(1, 1, "S")
         mm(0, 3)
-        t2(0, 0)
+        t1(0, 1)
         mm(1, 0)
+        linear(1, "G")
+        store_linear(0)
+        t2(0, 0)
+        mm(1, 1)
+        t2(0, 1)
         linear(2, "G")
         store_linear(1)
-        t2(0, 1)
-        mm(1, 1)
-        linear(3, "G")
         w_regroup(0, 1, "S")
-        store_linear(2)
         w_quant(1, 1)
         t1(0, 2)
-        linear(4, "G")
+        linear(3, "G")
+        store_linear(2)
         t1(0, 3)
-        store_linear(3)
         t2(0, 2)
         sin(0, 0)
-        linear(5, "G")
+        linear(4, "G")
+        store_linear(3)
         t2(0, 3)
-        store_linear(4)
         sin(0, 1)
         tr(0, 0)
         w_quant(0, 1)
         sin(0, 2)
         tr(0, 1)
+        linear(5, "G")
+        store_linear(4)
         t1(1, 0)
-        linear(6, "G")
-        store_linear(5)
         sin(0, 3)
         mm(1, 2)
         t1(1, 1)
         outc(0, 0, "S")
         mm(1, 3)
+        linear(6, "G")
         t2(1, 0)
-        linear(7, "G")
-        store_linear(6)
+        store_linear(5)
         outc(0, 1, "S")
         tr(0, 2)
         t2(1, 1)
         sin(1, 0)
         tr(0, 3)
         store(0, 0, 2)
+        linear(7, "G")
         t1(1, 2)
+        store_linear(6)
         sin(1, 1)
         mm(0, 4)
-        store_linear(7)
         t1(1, 3)
         outc(0, 2, "S")
         mm(0, 5)
         t2(1, 2)
+        store_linear(7)
         outc(0, 3, "S")
         tr(1, 0)
         t2(1, 3)

@@ -15,17 +15,27 @@ ACT = mybir.ActivationFunctionType
 
 FLOPS = 2 * 1024 * 1024 * 1024
 
-NP = 128
-B = 1024
-K = 1024
-N = 1024
-NT = B // NP
-NG = K // 512
-NJ = N // NP
-NHB = B // 512
+PARTS = 128
+ROWS = 1024
+K_DIM = 1024
+COLS = 1024
+BANK = 512
+X_TILES = ROWS // PARTS
+PASSES = K_DIM // BANK
+N_TILES = COLS // PARTS
+TILES_PER_HALF = BANK // PARTS
+X_HALVES = ROWS // BANK
+W_HALVES = COLS // BANK
 TURN = 1.0 / (2.0 * math.pi)
-GUARD = 1e-30
+TINY = 1e-30
 PI_BELOW = 3.1415925025939941
+SLOT = 16
+BANKS_AHEAD = 6
+
+BANK_ORDER = [
+    (h, j) for c in range(W_HALVES) for h in range(X_HALVES) for j in range(TILES_PER_HALF * c, TILES_PER_HALF * (c + 1))
+]
+PAIRS = len(BANK_ORDER) // 2
 
 
 def tile_time2vec_kernel(tc, x, W, P, w, p, sine_w, cosine_w, out):
@@ -33,403 +43,377 @@ def tile_time2vec_kernel(tc, x, W, P, w, p, sine_w, cosine_w, out):
     with ExitStack() as ctx:
         keep = ctx.enter_context(tc.tile_pool(name="keep", bufs=1))
         small = ctx.enter_context(tc.tile_pool(name="small", bufs=1))
-        linp = ctx.enter_context(tc.tile_pool(name="linp", bufs=8))
-        epi = ctx.enter_context(tc.tile_pool(name="epi", bufs=6))
+        flow = ctx.enter_context(tc.tile_pool(name="flow", bufs=BANKS_AHEAD))
         psum = ctx.enter_context(tc.psum_pool(name="psum", bufs=8))
 
-        x_view = x.rearrange("(p t) k -> p t k", t=NT)
-        out_view = out.rearrange("(p t) n -> p t n", t=NT)
-        w_view0 = W.rearrange("(g u q e) c -> g u q e c", g=NG, u=2, q=NP, e=2)
-        w_view1 = W.rearrange("(a q e) c -> e q a c", a=2 * NG, q=NP, e=2)
+        x_view = x.rearrange("(p t) k -> p t k", t=X_TILES)
+        out_view = out.rearrange("(p t) n -> p t n", t=X_TILES)
+        w_by_pass = W.rearrange("(g u q e) c -> g u q e c", g=PASSES, u=2, q=PARTS, e=2)
+        w_by_parity = W.rearrange("(a q e) c -> e q a c", a=2 * PASSES, q=PARTS, e=2)
 
-        def col(name):
-            return small.tile([NP, 1], F32, name=name)
+        def column(name):
+            return small.tile([PARTS, 1], F32, name=name)
 
-        srow = keep.tile([NP, 64], BF16)
-        ones = keep.tile([NP, NP], BF16)
-        prow = keep.tile([NP, NP], BF16)
-        warm = small.tile([NP, 1], F32)
-        junk = small.tile([NP, 1], F32)
-        ident = keep.tile([NP, NP], F32)
-        identb = keep.tile([NP, NP], BF16)
-        x_sb = [keep.tile([NP, 2, K], BF16, name="x_sb%d" % j) for j in range(NT // 2)]
-        w_raw = [[keep.tile([NP, 4, 512], BF16, name="w_raw%d%d" % (g, h)) for h in range(1)] for g in range(NG)]
-        w_raw1 = keep.tile([NP, NG, 4, 512], BF16)
-        sc32 = small.tile([NP, 4], F32)
-        w32 = sc32[:, 0:1]
-        p32 = sc32[:, 1:2]
-        sc32g = small.tile([NP, 2], F32)
-        sg2 = col("sg2")
-        cs1 = small.tile([NP, 2], F32)
-        c1 = cs1[:, 0:1]
-        s1 = cs1[:, 1:2]
-        ab = small.tile([NP, 2], F32)
-        den = col("den")
-        rden = col("rden")
-        ang = small.tile([NP, 2], F32)
-        sico = small.tile([NP, 2], F32)
-        tsin = small.tile([NP, 2], F32)
-        dd = col("dd")
-        nn = col("nn")
-        rdd = col("rdd")
-        tau = col("tau")
-        tau2 = col("tau2")
-        ca = col("ca")
-        cb = col("cb")
-        t4 = col("t4")
-        ga = col("ga")
-        gb = col("gb")
-        hh = col("hh")
-        gg = col("gg")
-        phi = col("phi")
-        beta = small.tile([NP, NJ], F32)
-        bturn = small.tile([NP, NJ], F32)
-        dsg = col("dsg")
-        amp = col("amp")
-        xg = [keep.tile([NP, NG, 512], BF16, name="xg%d" % t, align_bytes=64) for t in range(NT)]
-        xc = keep.tile([NP, NG, B], U32, align_bytes=64)
-        xs = keep.tile([NP, NG, B], U8, align_bytes=64)
-        wg = [[keep.tile([NP, 512, 4], BF16, name="wg%d%d" % (g, h), align_bytes=64) for h in range(2)] for g in range(NG)]
-        wc = keep.tile([NP, NG, N], U32, align_bytes=64)
-        ws = keep.tile([NP, NG, N], U8, align_bytes=64)
-        live = {}
-        scalars = (w, p, cosine_w, sine_w)
+        def pair(name):
+            return small.tile([PARTS, 2], F32, name=name)
 
-        def load_scalar(j):
-            nc.scalar.dma_start(out=srow[0:1, 16 * j : 16 * j + 1], in_=scalars[j].rearrange("(o n) -> o n", o=1))
+        scalar_row = keep.tile([PARTS, 4 * SLOT], BF16)
+        ones = keep.tile([PARTS, PARTS], BF16)
+        p_rows = keep.tile([PARTS, PARTS], BF16)
+        zero = column("zero")
+        unused = column("unused")
+        ident = keep.tile([PARTS, PARTS], F32)
+        ident_bf = keep.tile([PARTS, PARTS], BF16)
+        x_sb = [keep.tile([PARTS, 2, K_DIM], BF16, name="x_sb%d" % i) for i in range(X_TILES // 2)]
+        w_first = [keep.tile([PARTS, 4, BANK], BF16, name="w_first%d" % g) for g in range(PASSES)]
+        w_second = keep.tile([PARTS, PASSES, 4, BANK], BF16)
+        x_grouped = [keep.tile([PARTS, PASSES, BANK], BF16, name="x_grouped%d" % t, align_bytes=64) for t in range(X_TILES)]
+        x_codes = keep.tile([PARTS, PASSES, ROWS], U32, align_bytes=64)
+        x_scales = keep.tile([PARTS, PASSES, ROWS], U8, align_bytes=64)
+        w_grouped = [
+            [keep.tile([PARTS, BANK, 4], BF16, name="w_grouped%d%d" % (g, c), align_bytes=64) for c in range(W_HALVES)]
+            for g in range(PASSES)
+        ]
+        w_codes = keep.tile([PARTS, PASSES, COLS], U32, align_bytes=64)
+        w_scales = keep.tile([PARTS, PASSES, COLS], U8, align_bytes=64)
+        linear_out = [keep.tile([PARTS, K_DIM], F32, name="linear_out%d" % t) for t in range(X_TILES)]
+        periodic_out = [keep.tile([PARTS, TILES_PER_HALF, 2 * PARTS], F32, name="periodic_out%d" % i) for i in range(PAIRS)]
 
-        def load_p():
-            nc.scalar.dma_start(out=prow[0:NJ, :], in_=P.rearrange("(j n) -> j n", n=NP))
+        scalars = small.tile([PARTS, 4], F32)
+        w_and_p = pair("w_and_p")
+        twice_if_positive = column("twice_if_positive")
+        magnitudes = pair("magnitudes")
+        folded = pair("folded")
+        c1 = folded[:, 0:1]
+        s1 = folded[:, 1:2]
+        norm1 = column("norm1")
+        inv_norm1 = column("inv_norm1")
+        angles = pair("angles")
+        guess = angles[:, 0:1]
+        sin_cos = pair("sin_cos")
+        times_sin = pair("times_sin")
+        along = column("along")
+        across = column("across")
+        inv_along = column("inv_along")
+        signed_along = column("signed_along")
+        tan = column("tan")
+        tan2 = column("tan2")
+        tan4 = column("tan4")
+        atan_low = column("atan_low")
+        atan_high = column("atan_high")
+        root_low = column("root_low")
+        root_high = column("root_high")
+        atan_over_tan = column("atan_over_tan")
+        root = column("root")
+        phi = column("phi")
+        amp = column("amp")
+        bias_radians = small.tile([PARTS, N_TILES], F32)
+        bias_turns = small.tile([PARTS, N_TILES], F32)
 
-        def load_x(j):
-            nc.sync.dma_start(out=x_sb[j][:], in_=x_view[:, 2 * j : 2 * j + 2, :])
+        in_psum = {}
+        in_flow = {}
 
-        def load_w0(g, u):
-            nc.sync.dma_start(out=w_raw[g][0][:, 2 * u : 2 * u + 2, :], in_=w_view0[g, u][:, :, 0:512])
+        def load_scalar(i, scalar):
+            nc.scalar.dma_start(out=scalar_row[0:1, SLOT * i : SLOT * i + 1], in_=scalar.rearrange("(o n) -> o n", o=1))
 
-        def load_w1(e):
+        def load_x(i):
+            nc.sync.dma_start(out=x_sb[i][:], in_=x_view[:, 2 * i : 2 * i + 2, :])
+
+        def load_w_first(g, u):
+            nc.sync.dma_start(out=w_first[g][:, 2 * u : 2 * u + 2, :], in_=w_by_pass[g, u][:, :, 0:BANK])
+
+        def load_w_second(e):
             nc.sync.dma_start(
-                out=w_raw1[:].rearrange("p g (u e) c -> p (g u) e c", e=2)[:, :, e, :], in_=w_view1[e][:, :, 512:N]
+                out=w_second[:].rearrange("p g (u e) c -> p (g u) e c", e=2)[:, :, e, :], in_=w_by_parity[e][:, :, BANK:COLS]
             )
 
         def x_transpose(t):
-            xt = psum.tile([NP, 4, NP], F32, tag="bank", name="xt%d" % t)
-            xw = x_sb[t // 2][:, t % 2, :].bitcast(F32)
-            for j in range(4):
-                nc.tensor.transpose(out=xt[:, j, :], in_=xw[:, NP * j : NP * j + NP], identity=ident[:])
-            live[("xt", t)] = xt
+            words_t = psum.tile([PARTS, 4, PARTS], F32, tag="bank", name="words_t")
+            words = x_sb[t // 2][:, t % 2, :].bitcast(F32)
+            for a in range(4):
+                nc.tensor.transpose(out=words_t[:, a, :], in_=words[:, PARTS * a : PARTS * a + PARTS], identity=ident[:])
+            in_psum["x", t] = words_t
 
-        def x_copy(t, eng):
-            dst = xg[t][:].bitcast(F32).rearrange("p g (b u) -> p g b u", u=2)
-            src = live[("xt", t)][:].rearrange("p (g u) b -> p g b u", g=NG, u=2)
-            if eng == "S":
-                nc.scalar.copy(out=dst, in_=src)
-            else:
-                nc.vector.tensor_copy(out=dst, in_=src)
+        def x_copy(t):
+            nc.scalar.copy(
+                out=x_grouped[t][:].bitcast(F32).rearrange("p g (b u) -> p g b u", u=2),
+                in_=in_psum["x", t][:].rearrange("p (g u) b -> p g b u", g=PASSES, u=2),
+            )
 
         def x_quant(g, t):
-            nc.vector.quantize_mx(
-                out=xc[:, g, NP * t : NP * t + NP].bitcast(FP8X4), scales=xs[:, g, NP * t : NP * t + NP], in_=xg[t][:, g, :]
-            )
+            cols = slice(PARTS * t, PARTS * t + PARTS)
+            nc.vector.quantize_mx(out=x_codes[:, g, cols].bitcast(FP8X4), scales=x_scales[:, g, cols], in_=x_grouped[t][:, g, :])
 
-        def linear(t, eng):
-            lin = linp.tile([NP, K], F32, name="lin")
-            src = x_sb[t // 2][:, t % 2, :]
-            if eng == "S":
-                nc.scalar.activation(out=lin[:], in_=src, func=ACT.Identity, scale=w32, bias=p32)
-            elif eng == "G":
-                nc.gpsimd.tensor_scalar(out=lin[:], in0=src, scalar1=sc32g[:, 0:1], scalar2=sc32g[:, 1:2], op0=ALU.mult, op1=ALU.add)
-            else:
-                nc.vector.tensor_scalar(out=lin[:], in0=src, scalar1=w32, scalar2=p32, op0=ALU.mult, op1=ALU.add)
-            live[("lin", t)] = lin
-
-        def store_linear(t):
-            nc.sync.dma_start(out=out_view[:, t, 0:K], in_=live[("lin", t)][:])
-
-        def w_regroup(g, h, eng):
-            dst = wg[g][h][:].rearrange("p (c i) t -> p c t i", i=4)
-            raw = w_raw[g][0][:] if h == 0 else w_raw1[:, g]
-            src = raw.rearrange("p t (c i) -> p c t i", i=4)
-            if eng == "S":
-                nc.scalar.copy(out=dst, in_=src)
-            else:
+        def w_regroup(g, c):
+            rows = w_first[g][:] if c == 0 else w_second[:, g]
+            dst = w_grouped[g][c][:].rearrange("p (n i) t -> p n t i", i=4)
+            src = rows.rearrange("p t (n i) -> p n t i", i=4)
+            if c == 0:
                 nc.vector.tensor_copy(out=dst, in_=src)
+            else:
+                nc.scalar.copy(out=dst, in_=src)
 
-        def w_quant(g, h):
-            cols = slice(512 * h, 512 * h + 512)
+        def w_quant(g, c):
+            cols = slice(BANK * c, BANK * c + BANK)
             nc.vector.quantize_mx(
-                out=wc[:, g, cols].bitcast(FP8X4), scales=ws[:, g, cols], in_=wg[g][h][:].rearrange("p c t -> p (c t)")
+                out=w_codes[:, g, cols].bitcast(FP8X4),
+                scales=w_scales[:, g, cols],
+                in_=w_grouped[g][c][:].rearrange("p n t -> p (n t)"),
             )
 
-        def mm(hb, j):
-            z = psum.tile([NP, 512], F32, tag="bank", name="z")
-            for g in range(NG):
+        def linear(t):
+            nc.gpsimd.tensor_scalar(
+                out=linear_out[t][:],
+                in0=x_sb[t // 2][:, t % 2, :],
+                scalar1=w_and_p[:, 0:1],
+                scalar2=w_and_p[:, 1:2],
+                op0=ALU.mult,
+                op1=ALU.add,
+            )
+            nc.sync.dma_start(out=out_view[:, t, 0:K_DIM], in_=linear_out[t][:])
+
+        def spread_scalars():
+            spread = psum.tile([PARTS, 4, SLOT], F32, tag="bank", name="spread")
+            nc.tensor.matmul(out=spread[:].rearrange("p i s -> p (i s)"), lhsT=ones[:], rhs=scalar_row[:], start=True, stop=True)
+            in_psum["scalars"] = spread
+
+        def chain_fetch():
+            nc.vector.tensor_copy(out=scalars[:], in_=in_psum["scalars"][:, :, 0])
+
+        def chain_sign():
+            nc.vector.tensor_scalar(
+                out=twice_if_positive[:], in0=scalars[:, 3:4], scalar1=0.0, scalar2=2.0, op0=ALU.is_ge, op1=ALU.mult
+            )
+            nc.vector.scalar_tensor_tensor(
+                out=magnitudes[:], in0=scalars[:, 2:4], scalar=-1.0, in1=scalars[:, 2:4], op0=ALU.mult, op1=ALU.max
+            )
+
+        def chain_fold():
+            nc.vector.scalar_tensor_tensor(
+                out=folded[:], in0=scalars[:, 2:4], scalar=twice_if_positive[:], in1=scalars[:, 2:4], op0=ALU.mult, op1=ALU.subtract
+            )
+            nc.vector.tensor_scalar(
+                out=norm1[:], in0=magnitudes[:, 0:1], scalar1=magnitudes[:, 1:2], scalar2=TINY, op0=ALU.add, op1=ALU.add
+            )
+
+        def chain_invert_norm():
+            nc.vector.reciprocal(out=inv_norm1[:], in_=norm1[:])
+
+        def chain_guess():
+            nc.vector.tensor_scalar(out=guess, in0=c1, scalar1=inv_norm1[:], scalar2=0.5 * math.pi, op0=ALU.mult, op1=ALU.mult)
+
+        def chain_cos_argument():
+            nc.vector.tensor_scalar(
+                out=angles[:, 1:2], in0=guess, scalar1=0.5 * math.pi, scalar2=PI_BELOW, op0=ALU.add, op1=ALU.min
+            )
+
+        def chain_sin_cos():
+            nc.scalar.activation(out=sin_cos[:], in_=angles[:], func=ACT.Sin)
+
+        def chain_times_sin():
+            nc.vector.tensor_scalar(out=times_sin[:], in0=folded[:], scalar1=sin_cos[:, 0:1], scalar2=TINY, op0=ALU.mult, op1=ALU.add)
+
+        def chain_rotate():
+            nc.vector.scalar_tensor_tensor(
+                out=along[:], in0=s1, scalar=sin_cos[:, 1:2], in1=times_sin[:, 0:1], op0=ALU.mult, op1=ALU.add
+            )
+            nc.vector.scalar_tensor_tensor(
+                out=across[:], in0=c1, scalar=sin_cos[:, 1:2], in1=times_sin[:, 1:2], op0=ALU.mult, op1=ALU.subtract
+            )
+
+        def chain_invert_along():
+            nc.vector.reciprocal(out=inv_along[:], in_=along[:])
+            nc.vector.scalar_tensor_tensor(
+                out=signed_along[:], in0=along[:], scalar=twice_if_positive[:], in1=along[:], op0=ALU.mult, op1=ALU.subtract
+            )
+
+        def chain_tan():
+            nc.vector.tensor_scalar(out=tan[:], in0=across[:], scalar1=inv_along[:], scalar2=None, op0=ALU.mult)
+
+        def chain_tan2():
+            nc.vector.tensor_scalar(out=tan2[:], in0=tan[:], scalar1=tan[:], scalar2=None, op0=ALU.mult)
+
+        def chain_series_halves():
+            nc.vector.tensor_scalar(out=atan_low[:], in0=tan2[:], scalar1=-1.0 / 3.0, scalar2=1.0, op0=ALU.mult, op1=ALU.add)
+            nc.vector.tensor_scalar(out=atan_high[:], in0=tan2[:], scalar1=-1.0 / 7.0, scalar2=0.2, op0=ALU.mult, op1=ALU.add)
+            nc.vector.tensor_scalar(out=tan4[:], in0=tan2[:], scalar1=tan2[:], scalar2=None, op0=ALU.mult)
+            nc.vector.tensor_scalar(out=root_low[:], in0=tan2[:], scalar1=0.5, scalar2=1.0, op0=ALU.mult, op1=ALU.add)
+            nc.vector.tensor_scalar(out=root_high[:], in0=tan2[:], scalar1=1.0 / 16.0, scalar2=-0.125, op0=ALU.mult, op1=ALU.add)
+
+        def chain_series():
+            nc.vector.tensor_scalar(
+                out=atan_over_tan[:], in0=atan_high[:], scalar1=tan4[:], scalar2=atan_low[:], op0=ALU.mult, op1=ALU.add
+            )
+            nc.vector.tensor_scalar(out=root[:], in0=root_high[:], scalar1=tan4[:], scalar2=root_low[:], op0=ALU.mult, op1=ALU.add)
+
+        def chain_phi_amp():
+            nc.vector.tensor_scalar(out=phi[:], in0=atan_over_tan[:], scalar1=tan[:], scalar2=guess, op0=ALU.mult, op1=ALU.add)
+            nc.vector.tensor_scalar(out=amp[:], in0=root[:], scalar1=signed_along[:], scalar2=None, op0=ALU.mult)
+
+        def p_transpose():
+            p_t = psum.tile([PARTS, PARTS], BF16, tag="bank", name="p_t")
+            nc.tensor.transpose(out=p_t[:], in_=p_rows[:], identity=ident_bf[:])
+            in_psum["P"] = p_t
+
+        def chain_bias():
+            p_t = in_psum["P"][:, 0:N_TILES]
+            nc.vector.tensor_scalar(out=bias_radians[:], in0=p_t, scalar1=phi[:], scalar2=None, op0=ALU.add)
+            nc.vector.tensor_scalar(out=bias_turns[:], in0=p_t, scalar1=phi[:], scalar2=TURN, op0=ALU.add, op1=ALU.mult)
+
+        def multiply(bank):
+            h, j = bank
+            z = psum.tile([PARTS, BANK], F32, tag="bank", name="z")
+            n_cols = slice(PARTS * j, PARTS * j + PARTS)
+            b_cols = slice(BANK * h, BANK * h + BANK)
+            for g in range(PASSES):
                 nc.tensor.matmul_mx(
                     out=z[:],
-                    lhsT=wc[:, g, NP * j : NP * j + NP].bitcast(FP8X4),
-                    lhsT_scale=ws[:, g, NP * j : NP * j + NP],
-                    rhs=xc[:, g, 512 * hb : 512 * hb + 512].bitcast(FP8X4),
-                    rhs_scale=xs[:, g, 512 * hb : 512 * hb + 512],
+                    lhsT=w_codes[:, g, n_cols].bitcast(FP8X4),
+                    lhsT_scale=w_scales[:, g, n_cols],
+                    rhs=x_codes[:, g, b_cols].bitcast(FP8X4),
+                    rhs_scale=x_scales[:, g, b_cols],
                     start=(g == 0),
-                    stop=(g == NG - 1),
+                    stop=(g == PASSES - 1),
                 )
-            live[("z", hb, j)] = z
+            in_psum["z", bank] = z
 
-        def t1(hb, j):
-            ki = epi.tile([NP, 512], I32, name="ki")
+        def whole_turns(bank):
+            turns = flow.tile([PARTS, BANK], I32, name="turns")
             nc.vector.tensor_scalar(
-                out=ki[:], in0=live[("z", hb, j)][:], scalar1=TURN, scalar2=bturn[:, j : j + 1], op0=ALU.mult, op1=ALU.add
+                out=turns[:], in0=in_psum["z", bank][:], scalar1=TURN, scalar2=bias_turns[:, bank[1] : bank[1] + 1], op0=ALU.mult, op1=ALU.add
             )
-            live[("k", hb, j)] = ki
+            in_flow["turns", bank] = turns
 
-        def t2(hb, j):
-            fr = epi.tile([NP, 512], F32, name="fr")
+        def take_turns_off(bank):
+            rest = flow.tile([PARTS, BANK], F32, name="rest")
             nc.vector.scalar_tensor_tensor(
-                out=fr[:], in0=live[("z", hb, j)][:], scalar=TURN, in1=live[("k", hb, j)][:], op0=ALU.mult, op1=ALU.subtract
+                out=rest[:], in0=in_psum["z", bank][:], scalar=TURN, in1=in_flow["turns", bank][:], op0=ALU.mult, op1=ALU.subtract
             )
-            live[("f", hb, j)] = fr
+            in_flow["rest", bank] = rest
 
-        def sin(hb, j):
-            sn = epi.tile([NP, 512], F32, name="sn")
+        def sine(bank):
+            sines = flow.tile([PARTS, BANK], F32, name="sines")
             nc.scalar.activation(
-                out=sn[:], in_=live[("f", hb, j)][:], func=ACT.Sin, scale=2.0 * math.pi, bias=beta[:, j : j + 1]
+                out=sines[:], in_=in_flow["rest", bank][:], func=ACT.Sin, scale=2.0 * math.pi, bias=bias_radians[:, bank[1] : bank[1] + 1]
             )
-            live[("s", hb, j)] = sn
+            in_flow["sines", bank] = sines
 
-        def tr(hb, j):
-            ob = psum.tile([NP, 4, NP], F32, tag="bank", name="ob")
-            sn = live[("s", hb, j)]
-            for i in range(4):
-                nc.tensor.transpose(out=ob[:, i, :], in_=sn[:, NP * i : NP * i + NP], identity=ident[:])
-            live[("o", hb, j)] = ob
+        def transpose_back(bank):
+            sines_t = psum.tile([PARTS, TILES_PER_HALF, PARTS], F32, tag="bank", name="sines_t")
+            for i in range(TILES_PER_HALF):
+                nc.tensor.transpose(
+                    out=sines_t[:, i, :], in_=in_flow["sines", bank][:, PARTS * i : PARTS * i + PARTS], identity=ident[:]
+                )
+            in_psum["sines", bank] = sines_t
 
-        groups = [[[0,2],[2,4],[4,6],[6,8]],[[0,2],[2,4],[4,6],[6,8]]]
-
-        def outc(hb, j, eng):
-            j0, j1 = [gr for gr in groups[hb] if gr[0] <= j < gr[1]][0]
-            if ("st", hb, j0) not in live:
-                live[("st", hb, j0)] = keep.tile([NP, 4, NP * (j1 - j0)], F32, name="stage%d%d" % (hb, j0))
-            dst = live[("st", hb, j0)][:, :, NP * (j - j0) : NP * (j - j0) + NP]
-            if eng == "S":
-                nc.scalar.activation(out=dst, in_=live[("o", hb, j)][:], func=ACT.Copy, scale=amp[:])
+        def copy_out(position, on_vector):
+            dst = periodic_out[position // 2][:, :, PARTS * (position % 2) : PARTS * (position % 2) + PARTS]
+            src = in_psum["sines", BANK_ORDER[position]][:]
+            if on_vector:
+                nc.vector.tensor_scalar(out=dst, in0=src, scalar1=amp[:], scalar2=None, op0=ALU.mult)
             else:
-                nc.vector.tensor_scalar(out=dst, in0=live[("o", hb, j)][:], scalar1=amp[:], scalar2=None, op0=ALU.mult)
+                nc.scalar.activation(out=dst, in_=src, func=ACT.Copy, scale=amp[:])
 
-        def store(hb, j0, j1):
-            nc.sync.dma_start(out=out_view[:, 4 * hb : 4 * hb + 4, K + NP * j0 : K + NP * j1], in_=live[("st", hb, j0)][:])
+        def store_pair(i):
+            h, j = BANK_ORDER[2 * i]
+            nc.sync.dma_start(
+                out=out_view[:, TILES_PER_HALF * h : TILES_PER_HALF * h + TILES_PER_HALF, K_DIM + PARTS * j : K_DIM + PARTS * (j + 2)],
+                in_=periodic_out[i][:],
+            )
 
         ctx.enter_context(tc.manual_schedule())
-        nc.vector.memset(prow[:], 0.0)
-        nc.vector.memset(warm[:], 0.0)
-        nc.vector.memset(srow[:], 0.0)
+
+        nc.vector.memset(p_rows[:], 0.0)
+        nc.vector.memset(zero[:], 0.0)
+        nc.vector.memset(scalar_row[:], 0.0)
         nc.vector.memset(ones[:], 1.0)
-        sp = psum.tile([NP, 4, 16], F32, tag="bank", name="sp")
-        pt = psum.tile([NP, NP], BF16, tag="bank", name="pt")
-        load_scalar(0)
-        load_w0(0, 0)
+        for i, scalar in enumerate((w, p, cosine_w, sine_w)):
+            load_scalar(i, scalar)
+        nc.scalar.dma_start(out=p_rows[0:N_TILES, :], in_=P.rearrange("(j n) -> j n", n=PARTS))
+        nc.scalar.activation(out=unused[:], in_=zero[:], func=ACT.Sin)
         make_identity(nc, ident[:])
-        load_scalar(1)
-        load_w0(0, 1)
-        load_scalar(2)
+        nc.gpsimd.tensor_copy(out=ident_bf[:], in_=ident[:])
+        load_w_first(0, 0)
+        load_w_first(0, 1)
         load_x(0)
-        load_scalar(3)
-        load_w0(1, 0)
-        load_p()
-        load_w0(1, 1)
-        nc.scalar.activation(out=junk[:], in_=warm[:], func=ACT.Sin)
+        load_w_first(1, 0)
+        load_w_first(1, 1)
         load_x(1)
         load_x(2)
         load_x(3)
-        load_w1(0)
-        load_w1(1)
-        nc.gpsimd.tensor_copy(out=identb[:], in_=ident[:])
-        nc.tensor.matmul(out=sp[:].rearrange("p j k -> p (j k)"), lhsT=ones[:], rhs=srow[:], start=True, stop=True)
-        w_regroup(0, 0, "V")
-        nc.vector.tensor_copy(out=sc32[:], in_=sp[:, :, 0])
-        x_transpose(0)
-        nc.vector.tensor_scalar(out=sg2[:], in0=sc32[:, 3:4], scalar1=0.0, scalar2=2.0, op0=ALU.is_ge, op1=ALU.mult)
-        nc.vector.scalar_tensor_tensor(out=ab[:], in0=sc32[:, 2:4], scalar=-1.0, in1=sc32[:, 2:4], op0=ALU.mult, op1=ALU.max)
+        load_w_second(0)
+        load_w_second(1)
+
+        spread_scalars()
+        for t in range(2):
+            x_transpose(t)
+            x_copy(t)
+        w_regroup(0, 0)
+        chain_fetch()
+        chain_sign()
         w_quant(0, 0)
-        x_transpose(1)
-        x_copy(0, "S")
-        nc.vector.scalar_tensor_tensor(out=cs1[:], in0=sc32[:, 2:4], scalar=sg2[:], in1=sc32[:, 2:4], op0=ALU.mult, op1=ALU.subtract)
-        nc.vector.tensor_scalar(out=den[:], in0=ab[:, 0:1], scalar1=ab[:, 1:2], scalar2=GUARD, op0=ALU.add, op1=ALU.add)
-        x_copy(1, "S")
-        nc.vector.reciprocal(out=rden[:], in_=den[:])
-        w_regroup(1, 0, "V")
-        nc.vector.tensor_scalar(out=ang[:, 0:1], in0=c1, scalar1=rden[:], scalar2=0.5 * math.pi, op0=ALU.mult, op1=ALU.mult)
-        x_transpose(2)
-        nc.vector.tensor_scalar(out=ang[:, 1:2], in0=ang[:, 0:1], scalar1=0.5 * math.pi, scalar2=PI_BELOW, op0=ALU.add, op1=ALU.min)
+        chain_fold()
+        chain_invert_norm()
+        w_regroup(1, 0)
+        chain_guess()
+        chain_cos_argument()
+        chain_sin_cos()
+        for t in range(2, X_TILES):
+            x_transpose(t)
+            if t == 3:
+                p_transpose()
+            x_copy(t)
         x_quant(0, 0)
-        nc.scalar.activation(out=sico[:], in_=ang[:], func=ACT.Sin)
-        x_transpose(3)
         x_quant(1, 0)
-        x_copy(2, "S")
         w_quant(1, 0)
-        nc.tensor.transpose(out=pt[:], in_=prow[:], identity=identb[:])
-        x_copy(3, "S")
-        nc.vector.tensor_scalar(out=tsin[:], in0=cs1[:], scalar1=sico[:, 0:1], scalar2=GUARD, op0=ALU.mult, op1=ALU.add)
-        x_transpose(4)
-        x_quant(0, 1)
-        x_quant(1, 1)
-        nc.vector.scalar_tensor_tensor(out=dd[:], in0=s1, scalar=sico[:, 1:2], in1=tsin[:, 0:1], op0=ALU.mult, op1=ALU.add)
-        x_transpose(5)
-        nc.vector.scalar_tensor_tensor(out=nn[:], in0=c1, scalar=sico[:, 1:2], in1=tsin[:, 1:2], op0=ALU.mult, op1=ALU.subtract)
-        x_copy(4, "S")
-        x_quant(0, 2)
-        x_quant(1, 2)
-        nc.vector.reciprocal(out=rdd[:], in_=dd[:])
-        nc.vector.scalar_tensor_tensor(out=dsg[:], in0=dd[:], scalar=sg2[:], in1=dd[:], op0=ALU.mult, op1=ALU.subtract)
-        x_quant(0, 3)
-        x_copy(5, "S")
-        x_quant(1, 3)
-        x_transpose(6)
-        nc.vector.tensor_scalar(out=tau[:], in0=nn[:], scalar1=rdd[:], scalar2=None, op0=ALU.mult)
-        x_quant(0, 4)
-        x_transpose(7)
-        nc.vector.tensor_scalar(out=tau2[:], in0=tau[:], scalar1=tau[:], scalar2=None, op0=ALU.mult)
-        x_quant(1, 4)
-        x_copy(6, "S")
-        nc.vector.tensor_scalar(out=ca[:], in0=tau2[:], scalar1=-1.0 / 3.0, scalar2=1.0, op0=ALU.mult, op1=ALU.add)
-        nc.vector.tensor_scalar(out=cb[:], in0=tau2[:], scalar1=-1.0 / 7.0, scalar2=0.2, op0=ALU.mult, op1=ALU.add)
-        mm(0, 0)
-        nc.vector.tensor_scalar(out=t4[:], in0=tau2[:], scalar1=tau2[:], scalar2=None, op0=ALU.mult)
-        nc.vector.tensor_scalar(out=ga[:], in0=tau2[:], scalar1=0.5, scalar2=1.0, op0=ALU.mult, op1=ALU.add)
-        nc.vector.tensor_scalar(out=gb[:], in0=tau2[:], scalar1=1.0 / 16.0, scalar2=-0.125, op0=ALU.mult, op1=ALU.add)
-        x_quant(0, 5)
-        x_copy(7, "S")
-        nc.vector.tensor_scalar(out=hh[:], in0=cb[:], scalar1=t4[:], scalar2=ca[:], op0=ALU.mult, op1=ALU.add)
-        nc.vector.tensor_scalar(out=gg[:], in0=gb[:], scalar1=t4[:], scalar2=ga[:], op0=ALU.mult, op1=ALU.add)
-        x_quant(1, 5)
-        mm(0, 1)
-        nc.vector.tensor_scalar(out=phi[:], in0=hh[:], scalar1=tau[:], scalar2=ang[:, 0:1], op0=ALU.mult, op1=ALU.add)
-        nc.vector.tensor_scalar(out=amp[:], in0=gg[:], scalar1=dsg[:], scalar2=None, op0=ALU.mult)
-        x_quant(0, 6)
-        nc.vector.tensor_scalar(out=beta[:], in0=pt[:, 0:NJ], scalar1=phi[:], scalar2=None, op0=ALU.add)
-        nc.vector.tensor_scalar(out=bturn[:], in0=pt[:, 0:NJ], scalar1=phi[:], scalar2=TURN, op0=ALU.add, op1=ALU.mult)
-        nc.vector.tensor_copy(out=sc32g[:], in_=sc32[:, 0:2])
-        mm(0, 2)
-        x_quant(1, 6)
-        linear(0, "G")
-        x_quant(0, 7)
-        x_quant(1, 7)
-        t1(0, 0)
-        w_regroup(1, 1, "S")
-        mm(0, 3)
-        t1(0, 1)
-        mm(1, 0)
-        linear(1, "G")
-        store_linear(0)
-        t2(0, 0)
-        mm(1, 1)
-        t2(0, 1)
-        linear(2, "G")
-        store_linear(1)
-        w_regroup(0, 1, "S")
-        w_quant(1, 1)
-        t1(0, 2)
-        linear(3, "G")
-        store_linear(2)
-        t1(0, 3)
-        t2(0, 2)
-        sin(0, 0)
-        linear(4, "G")
-        store_linear(3)
-        t2(0, 3)
-        sin(0, 1)
-        tr(0, 0)
-        w_quant(0, 1)
-        sin(0, 2)
-        tr(0, 1)
-        linear(5, "G")
-        store_linear(4)
-        t1(1, 0)
-        sin(0, 3)
-        mm(1, 2)
-        t1(1, 1)
-        outc(0, 0, "S")
-        mm(1, 3)
-        linear(6, "G")
-        t2(1, 0)
-        store_linear(5)
-        outc(0, 1, "S")
-        tr(0, 2)
-        t2(1, 1)
-        sin(1, 0)
-        tr(0, 3)
-        store(0, 0, 2)
-        linear(7, "G")
-        t1(1, 2)
-        store_linear(6)
-        sin(1, 1)
-        mm(0, 4)
-        t1(1, 3)
-        outc(0, 2, "S")
-        mm(0, 5)
-        t2(1, 2)
-        store_linear(7)
-        outc(0, 3, "S")
-        tr(1, 0)
-        t2(1, 3)
-        sin(1, 2)
-        tr(1, 1)
-        store(0, 2, 4)
-        t1(0, 4)
-        mm(0, 6)
-        sin(1, 3)
-        t1(0, 5)
-        outc(1, 0, "S")
-        mm(0, 7)
-        t2(0, 4)
-        outc(1, 1, "S")
-        tr(1, 2)
-        t2(0, 5)
-        sin(0, 4)
-        tr(1, 3)
-        store(1, 0, 2)
-        t1(0, 6)
-        mm(1, 4)
-        sin(0, 5)
-        t1(0, 7)
-        outc(1, 2, "S")
-        mm(1, 5)
-        t2(0, 6)
-        outc(1, 3, "S")
-        tr(0, 4)
-        t2(0, 7)
-        sin(0, 6)
-        tr(0, 5)
-        store(1, 2, 4)
-        t1(1, 4)
-        mm(1, 6)
-        sin(0, 7)
-        t1(1, 5)
-        outc(0, 4, "S")
-        mm(1, 7)
-        t2(1, 4)
-        outc(0, 5, "S")
-        tr(0, 6)
-        t2(1, 5)
-        sin(1, 4)
-        tr(0, 7)
-        store(0, 4, 6)
-        t1(1, 6)
-        sin(1, 5)
-        tr(1, 4)
-        t1(1, 7)
-        outc(0, 6, "S")
-        tr(1, 5)
-        t2(1, 6)
-        outc(0, 7, "S")
-        t2(1, 7)
-        sin(1, 6)
-        store(0, 6, 8)
-        outc(1, 4, "V")
-        sin(1, 7)
-        tr(1, 6)
-        outc(1, 5, "V")
-        tr(1, 7)
-        outc(1, 6, "S")
-        store(1, 4, 6)
-        outc(1, 7, "V")
-        store(1, 6, 8)
+        chain_rest = [
+            chain_times_sin,
+            chain_rotate,
+            chain_invert_along,
+            chain_tan,
+            chain_tan2,
+            chain_series_halves,
+            chain_series,
+            chain_phi_amp,
+            chain_bias,
+        ]
+        x_quants = [(g, t) for t in range(1, X_TILES) for g in range(PASSES)]
+        for i, (g, t) in enumerate(x_quants):
+            if i < len(chain_rest):
+                chain_rest[i]()
+            x_quant(g, t)
+
+        nc.vector.tensor_copy(out=w_and_p[:], in_=scalars[:, 0:2])
+        for t in range(X_TILES):
+            linear(t)
+        w_regroup(1, 1)
+        w_regroup(0, 1)
+        for position in range(BANKS_AHEAD):
+            multiply(BANK_ORDER[position])
+
+        for i in range(PAIRS):
+            first, second = BANK_ORDER[2 * i], BANK_ORDER[2 * i + 1]
+            whole_turns(first)
+            whole_turns(second)
+            take_turns_off(first)
+            take_turns_off(second)
+            if i == 1:
+                w_quant(1, 1)
+                w_quant(0, 1)
+            sine(first)
+            sine(second)
+            if 1 <= i < PAIRS - 1:
+                copy_out(2 * i - 2, False)
+                copy_out(2 * i - 1, False)
+                store_pair(i - 1)
+            transpose_back(first)
+            transpose_back(second)
+            for position in range(2 * i + BANKS_AHEAD, min(2 * i + BANKS_AHEAD + 2, len(BANK_ORDER))):
+                multiply(BANK_ORDER[position])
+
+        copy_out(2 * PAIRS - 4, True)
+        copy_out(2 * PAIRS - 3, True)
+        store_pair(PAIRS - 2)
+        copy_out(2 * PAIRS - 2, False)
+        copy_out(2 * PAIRS - 1, True)
+        store_pair(PAIRS - 1)

@@ -19,13 +19,17 @@ PARTS = 128
 ROWS = 1024
 K_DIM = 1024
 COLS = 1024
+PACK = 4
+K_PASS = PARTS * PACK
 BANK = 512
+HALF_COLS = COLS // 2
 X_TILES = ROWS // PARTS
-PASSES = K_DIM // BANK
+PASSES = K_DIM // K_PASS
 N_TILES = COLS // PARTS
 TILES_PER_HALF = BANK // PARTS
 X_HALVES = ROWS // BANK
-W_HALVES = COLS // BANK
+W_HALVES = COLS // HALF_COLS
+N_TILES_PER_HALF = HALF_COLS // PARTS
 TURN = 1.0 / (2.0 * math.pi)
 TINY = 1e-30
 PI_BELOW = 3.1415925025939941
@@ -33,7 +37,7 @@ SLOT = 16
 BANKS_AHEAD = 6
 
 BANK_ORDER = [
-    (h, j) for c in range(W_HALVES) for h in range(X_HALVES) for j in range(TILES_PER_HALF * c, TILES_PER_HALF * (c + 1))
+    (h, j) for c in range(W_HALVES) for h in range(X_HALVES) for j in range(N_TILES_PER_HALF * c, N_TILES_PER_HALF * (c + 1))
 ]
 PAIRS = len(BANK_ORDER) // 2
 
@@ -46,15 +50,15 @@ def tile_time2vec_kernel(tc, x, W, P, w, p, sine_w, cosine_w, out):
         flow = ctx.enter_context(tc.tile_pool(name="flow", bufs=BANKS_AHEAD))
         psum = ctx.enter_context(tc.psum_pool(name="psum", bufs=8))
 
-        x_view = x.rearrange("(p t) k -> p t k", t=X_TILES)
-        out_view = out.rearrange("(p t) n -> p t n", t=X_TILES)
+        x_view = x.rearrange("(q t) k -> q t k", t=X_TILES)
+        out_view = out.rearrange("(q t) n -> q t n", t=X_TILES)
         w_by_pass = W.rearrange("(g u q e) c -> g u q e c", g=PASSES, u=2, q=PARTS, e=2)
         w_by_parity = W.rearrange("(a q e) c -> e q a c", a=2 * PASSES, q=PARTS, e=2)
 
         def column(name):
             return small.tile([PARTS, 1], F32, name=name)
 
-        def pair(name):
+        def two_columns(name):
             return small.tile([PARTS, 2], F32, name=name)
 
         scalar_row = keep.tile([PARTS, 4 * SLOT], BF16)
@@ -64,34 +68,38 @@ def tile_time2vec_kernel(tc, x, W, P, w, p, sine_w, cosine_w, out):
         unused = column("unused")
         ident = keep.tile([PARTS, PARTS], F32)
         ident_bf = keep.tile([PARTS, PARTS], BF16)
-        x_sb = [keep.tile([PARTS, 2, K_DIM], BF16, name="x_sb%d" % i) for i in range(X_TILES // 2)]
-        w_first = [keep.tile([PARTS, 4, BANK], BF16, name="w_first%d" % g) for g in range(PASSES)]
-        w_second = keep.tile([PARTS, PASSES, 4, BANK], BF16)
-        x_grouped = [keep.tile([PARTS, PASSES, BANK], BF16, name="x_grouped%d" % t, align_bytes=64) for t in range(X_TILES)]
+        x_sb = [keep.tile([PARTS, 2, K_DIM], BF16, name="x_sb%d" % d) for d in range(X_TILES // 2)]
+        w_first = [keep.tile([PARTS, PACK, HALF_COLS], BF16, name="w_first%d" % g) for g in range(PASSES)]
+        w_second = keep.tile([PARTS, PASSES, PACK, HALF_COLS], BF16)
+        x_grouped = [
+            keep.tile([PARTS, PASSES, PARTS * PACK], BF16, name="x_grouped%d" % t, align_bytes=64) for t in range(X_TILES)
+        ]
         x_codes = keep.tile([PARTS, PASSES, ROWS], U32, align_bytes=64)
         x_scales = keep.tile([PARTS, PASSES, ROWS], U8, align_bytes=64)
         w_grouped = [
-            [keep.tile([PARTS, BANK, 4], BF16, name="w_grouped%d%d" % (g, c), align_bytes=64) for c in range(W_HALVES)]
+            [keep.tile([PARTS, HALF_COLS, PACK], BF16, name="w_grouped%d%d" % (g, c), align_bytes=64) for c in range(W_HALVES)]
             for g in range(PASSES)
         ]
         w_codes = keep.tile([PARTS, PASSES, COLS], U32, align_bytes=64)
         w_scales = keep.tile([PARTS, PASSES, COLS], U8, align_bytes=64)
         linear_out = [keep.tile([PARTS, K_DIM], F32, name="linear_out%d" % t) for t in range(X_TILES)]
-        periodic_out = [keep.tile([PARTS, TILES_PER_HALF, 2 * PARTS], F32, name="periodic_out%d" % i) for i in range(PAIRS)]
+        periodic_out = [
+            keep.tile([PARTS, TILES_PER_HALF, 2 * PARTS], F32, name="periodic_out%d" % number) for number in range(PAIRS)
+        ]
 
         scalars = small.tile([PARTS, 4], F32)
-        w_and_p = pair("w_and_p")
+        w_and_p = two_columns("w_and_p")
         twice_if_positive = column("twice_if_positive")
-        magnitudes = pair("magnitudes")
-        folded = pair("folded")
+        magnitudes = two_columns("magnitudes")
+        folded = two_columns("folded")
         c1 = folded[:, 0:1]
         s1 = folded[:, 1:2]
         norm1 = column("norm1")
         inv_norm1 = column("inv_norm1")
-        angles = pair("angles")
+        angles = two_columns("angles")
         guess = angles[:, 0:1]
-        sin_cos = pair("sin_cos")
-        times_sin = pair("times_sin")
+        sin_cos = two_columns("sin_cos")
+        times_sin = two_columns("times_sin")
         along = column("along")
         across = column("across")
         inv_along = column("inv_along")
@@ -110,34 +118,38 @@ def tile_time2vec_kernel(tc, x, W, P, w, p, sine_w, cosine_w, out):
         bias_radians = small.tile([PARTS, N_TILES], F32)
         bias_turns = small.tile([PARTS, N_TILES], F32)
 
+        spread = psum.tile([PARTS, 4, SLOT], F32, tag="bank", name="spread")
+        p_t = psum.tile([PARTS, PARTS], BF16, tag="bank", name="p_t")
         in_psum = {}
         in_flow = {}
 
-        def load_scalar(i, scalar):
-            nc.scalar.dma_start(out=scalar_row[0:1, SLOT * i : SLOT * i + 1], in_=scalar.rearrange("(o n) -> o n", o=1))
+        def load_scalar(place, scalar):
+            nc.scalar.dma_start(
+                out=scalar_row[0:1, SLOT * place : SLOT * place + 1], in_=scalar.rearrange("(o v) -> o v", o=1)
+            )
 
-        def load_x(i):
-            nc.sync.dma_start(out=x_sb[i][:], in_=x_view[:, 2 * i : 2 * i + 2, :])
+        def load_x(d):
+            nc.sync.dma_start(out=x_sb[d][:], in_=x_view[:, 2 * d : 2 * d + 2, :])
 
         def load_w_first(g, u):
-            nc.sync.dma_start(out=w_first[g][:, 2 * u : 2 * u + 2, :], in_=w_by_pass[g, u][:, :, 0:BANK])
+            nc.sync.dma_start(out=w_first[g][:, 2 * u : 2 * u + 2, :], in_=w_by_pass[g, u][:, :, 0:HALF_COLS])
 
         def load_w_second(e):
             nc.sync.dma_start(
-                out=w_second[:].rearrange("p g (u e) c -> p (g u) e c", e=2)[:, :, e, :], in_=w_by_parity[e][:, :, BANK:COLS]
+                out=w_second[:].rearrange("q g (u e) c -> q (g u) e c", e=2)[:, :, e, :], in_=w_by_parity[e][:, :, HALF_COLS:COLS]
             )
 
         def x_transpose(t):
-            words_t = psum.tile([PARTS, 4, PARTS], F32, tag="bank", name="words_t")
+            words_t = psum.tile([PARTS, 2 * PASSES, PARTS], F32, tag="bank", name="words_t")
             words = x_sb[t // 2][:, t % 2, :].bitcast(F32)
-            for a in range(4):
+            for a in range(2 * PASSES):
                 nc.tensor.transpose(out=words_t[:, a, :], in_=words[:, PARTS * a : PARTS * a + PARTS], identity=ident[:])
             in_psum["x", t] = words_t
 
         def x_copy(t):
             nc.scalar.copy(
-                out=x_grouped[t][:].bitcast(F32).rearrange("p g (b u) -> p g b u", u=2),
-                in_=in_psum["x", t][:].rearrange("p (g u) b -> p g b u", g=PASSES, u=2),
+                out=x_grouped[t][:].bitcast(F32).rearrange("q g (b u) -> q g b u", u=2),
+                in_=in_psum["x", t][:].rearrange("q (g u) b -> q g b u", g=PASSES, u=2),
             )
 
         def x_quant(g, t):
@@ -146,19 +158,19 @@ def tile_time2vec_kernel(tc, x, W, P, w, p, sine_w, cosine_w, out):
 
         def w_regroup(g, c):
             rows = w_first[g][:] if c == 0 else w_second[:, g]
-            dst = w_grouped[g][c][:].rearrange("p (n i) t -> p n t i", i=4)
-            src = rows.rearrange("p t (n i) -> p n t i", i=4)
+            dst = w_grouped[g][c][:].rearrange("q (n r) y -> q n y r", r=4)
+            src = rows.rearrange("q y (n r) -> q n y r", r=4)
             if c == 0:
                 nc.vector.tensor_copy(out=dst, in_=src)
             else:
                 nc.scalar.copy(out=dst, in_=src)
 
         def w_quant(g, c):
-            cols = slice(BANK * c, BANK * c + BANK)
+            cols = slice(HALF_COLS * c, HALF_COLS * c + HALF_COLS)
             nc.vector.quantize_mx(
                 out=w_codes[:, g, cols].bitcast(FP8X4),
                 scales=w_scales[:, g, cols],
-                in_=w_grouped[g][c][:].rearrange("p n t -> p (n t)"),
+                in_=w_grouped[g][c][:].rearrange("q n y -> q (n y)"),
             )
 
         def linear(t):
@@ -170,15 +182,20 @@ def tile_time2vec_kernel(tc, x, W, P, w, p, sine_w, cosine_w, out):
                 op0=ALU.mult,
                 op1=ALU.add,
             )
+
+        def store_linear(t):
             nc.sync.dma_start(out=out_view[:, t, 0:K_DIM], in_=linear_out[t][:])
 
+        def hand_w_and_p_to_gpsimd():
+            nc.vector.tensor_copy(out=w_and_p[:], in_=scalars[:, 0:2])
+
         def spread_scalars():
-            spread = psum.tile([PARTS, 4, SLOT], F32, tag="bank", name="spread")
-            nc.tensor.matmul(out=spread[:].rearrange("p i s -> p (i s)"), lhsT=ones[:], rhs=scalar_row[:], start=True, stop=True)
-            in_psum["scalars"] = spread
+            nc.tensor.matmul(
+                out=spread[:].rearrange("q l s -> q (l s)"), lhsT=ones[:], rhs=scalar_row[:], start=True, stop=True
+            )
 
         def chain_fetch():
-            nc.vector.tensor_copy(out=scalars[:], in_=in_psum["scalars"][:, :, 0])
+            nc.vector.tensor_copy(out=scalars[:], in_=spread[:, :, 0])
 
         def chain_sign():
             nc.vector.tensor_scalar(
@@ -251,14 +268,13 @@ def tile_time2vec_kernel(tc, x, W, P, w, p, sine_w, cosine_w, out):
             nc.vector.tensor_scalar(out=amp[:], in0=root[:], scalar1=signed_along[:], scalar2=None, op0=ALU.mult)
 
         def p_transpose():
-            p_t = psum.tile([PARTS, PARTS], BF16, tag="bank", name="p_t")
             nc.tensor.transpose(out=p_t[:], in_=p_rows[:], identity=ident_bf[:])
-            in_psum["P"] = p_t
 
         def chain_bias():
-            p_t = in_psum["P"][:, 0:N_TILES]
-            nc.vector.tensor_scalar(out=bias_radians[:], in0=p_t, scalar1=phi[:], scalar2=None, op0=ALU.add)
-            nc.vector.tensor_scalar(out=bias_turns[:], in0=p_t, scalar1=phi[:], scalar2=TURN, op0=ALU.add, op1=ALU.mult)
+            nc.vector.tensor_scalar(out=bias_radians[:], in0=p_t[:, 0:N_TILES], scalar1=phi[:], scalar2=None, op0=ALU.add)
+            nc.vector.tensor_scalar(
+                out=bias_turns[:], in0=p_t[:, 0:N_TILES], scalar1=phi[:], scalar2=TURN, op0=ALU.add, op1=ALU.mult
+            )
 
         def multiply(bank):
             h, j = bank
@@ -300,9 +316,11 @@ def tile_time2vec_kernel(tc, x, W, P, w, p, sine_w, cosine_w, out):
 
         def transpose_back(bank):
             sines_t = psum.tile([PARTS, TILES_PER_HALF, PARTS], F32, tag="bank", name="sines_t")
-            for i in range(TILES_PER_HALF):
+            for member in range(TILES_PER_HALF):
                 nc.tensor.transpose(
-                    out=sines_t[:, i, :], in_=in_flow["sines", bank][:, PARTS * i : PARTS * i + PARTS], identity=ident[:]
+                    out=sines_t[:, member, :],
+                    in_=in_flow["sines", bank][:, PARTS * member : PARTS * member + PARTS],
+                    identity=ident[:],
                 )
             in_psum["sines", bank] = sines_t
 
@@ -314,11 +332,11 @@ def tile_time2vec_kernel(tc, x, W, P, w, p, sine_w, cosine_w, out):
             else:
                 nc.scalar.activation(out=dst, in_=src, func=ACT.Copy, scale=amp[:])
 
-        def store_pair(i):
-            h, j = BANK_ORDER[2 * i]
+        def store_pair(number):
+            h, j = BANK_ORDER[2 * number]
             nc.sync.dma_start(
                 out=out_view[:, TILES_PER_HALF * h : TILES_PER_HALF * h + TILES_PER_HALF, K_DIM + PARTS * j : K_DIM + PARTS * (j + 2)],
-                in_=periodic_out[i][:],
+                in_=periodic_out[number][:],
             )
 
         ctx.enter_context(tc.manual_schedule())
@@ -327,9 +345,9 @@ def tile_time2vec_kernel(tc, x, W, P, w, p, sine_w, cosine_w, out):
         nc.vector.memset(zero[:], 0.0)
         nc.vector.memset(scalar_row[:], 0.0)
         nc.vector.memset(ones[:], 1.0)
-        for i, scalar in enumerate((w, p, cosine_w, sine_w)):
-            load_scalar(i, scalar)
-        nc.scalar.dma_start(out=p_rows[0:N_TILES, :], in_=P.rearrange("(j n) -> j n", n=PARTS))
+        for place, scalar in enumerate((w, p, cosine_w, sine_w)):
+            load_scalar(place, scalar)
+        nc.scalar.dma_start(out=p_rows[0:N_TILES, :], in_=P.rearrange("(j q) -> j q", q=PARTS))
         nc.scalar.activation(out=unused[:], in_=zero[:], func=ACT.Sin)
         make_identity(nc, ident[:])
         nc.gpsimd.tensor_copy(out=ident_bf[:], in_=ident[:])
@@ -378,37 +396,42 @@ def tile_time2vec_kernel(tc, x, W, P, w, p, sine_w, cosine_w, out):
             chain_bias,
         ]
         x_quants = [(g, t) for t in range(1, X_TILES) for g in range(PASSES)]
-        for i, (g, t) in enumerate(x_quants):
-            if i < len(chain_rest):
-                chain_rest[i]()
+        step_before = [0, 2, 4, 6, 7, 8, 9, 10, 11]
+        for count, (g, t) in enumerate(x_quants):
+            if count in step_before:
+                chain_rest[step_before.index(count)]()
+            if count == step_before[-1]:
+                hand_w_and_p_to_gpsimd()
             x_quant(g, t)
-
-        nc.vector.tensor_copy(out=w_and_p[:], in_=scalars[:, 0:2])
         for t in range(X_TILES):
             linear(t)
+        for t in range(X_TILES - 2):
+            store_linear(t)
         w_regroup(1, 1)
         w_regroup(0, 1)
         for position in range(BANKS_AHEAD):
             multiply(BANK_ORDER[position])
 
-        for i in range(PAIRS):
-            first, second = BANK_ORDER[2 * i], BANK_ORDER[2 * i + 1]
+        for number in range(PAIRS):
+            first, second = BANK_ORDER[2 * number], BANK_ORDER[2 * number + 1]
             whole_turns(first)
             whole_turns(second)
             take_turns_off(first)
             take_turns_off(second)
-            if i == 1:
-                w_quant(1, 1)
-                w_quant(0, 1)
+            if number < PASSES:
+                w_quant(PASSES - 1 - number, 1)
             sine(first)
             sine(second)
-            if 1 <= i < PAIRS - 1:
-                copy_out(2 * i - 2, False)
-                copy_out(2 * i - 1, False)
-                store_pair(i - 1)
+            if 1 <= number < PAIRS - 1:
+                copy_out(2 * number - 2, False)
+                copy_out(2 * number - 1, False)
+                store_pair(number - 1)
+            if number == 1:
+                store_linear(X_TILES - 2)
+                store_linear(X_TILES - 1)
             transpose_back(first)
             transpose_back(second)
-            for position in range(2 * i + BANKS_AHEAD, min(2 * i + BANKS_AHEAD + 2, len(BANK_ORDER))):
+            for position in range(2 * number + BANKS_AHEAD, min(2 * number + BANKS_AHEAD + 2, len(BANK_ORDER))):
                 multiply(BANK_ORDER[position])
 
         copy_out(2 * PAIRS - 4, True)

import math
from contextlib import ExitStack

import concourse.mybir as mybir
from concourse.masks import make_identity

F32 = mybir.dt.float32
BF16 = mybir.dt.bfloat16
I32 = mybir.dt.int32
U32 = mybir.dt.uint32
U8 = mybir.dt.uint8
FP8X4 = mybir.dt.float8_e4m3fn_x4
ALU = mybir.AluOpType
ACT = mybir.ActivationFunctionType

FLOPS = 2 * 1024 * 1024 * 1024

PARTS = 128
ROWS = 1024
K_DIM = 1024
COLS = 1024
PACK = 4
K_PASS = PARTS * PACK
BANK = 512
HALF_COLS = COLS // 2
X_TILES = ROWS // PARTS
PASSES = K_DIM // K_PASS
N_TILES = COLS // PARTS
TILES_PER_HALF = BANK // PARTS
X_HALVES = ROWS // BANK
W_HALVES = COLS // HALF_COLS
N_TILES_PER_HALF = HALF_COLS // PARTS
TURN = 1.0 / (2.0 * math.pi)
TINY = 1e-30
PI_BELOW = 3.1415925025939941
SLOT = 16
BANKS_AHEAD = 6

BANK_ORDER = [
    (h, j) for c in range(W_HALVES) for h in range(X_HALVES) for j in range(N_TILES_PER_HALF * c, N_TILES_PER_HALF * (c + 1))
]
PAIRS = len(BANK_ORDER) // 2


def tile_time2vec_kernel(tc, x, W, P, w, p, sine_w, cosine_w, out):
    nc = tc.nc
    with ExitStack() as ctx:
        keep = ctx.enter_context(tc.tile_pool(name="keep", bufs=1))
        small = ctx.enter_context(tc.tile_pool(name="small", bufs=1))
        flow = ctx.enter_context(tc.tile_pool(name="flow", bufs=BANKS_AHEAD))
        psum = ctx.enter_context(tc.psum_pool(name="psum", bufs=8))

        x_view = x.rearrange("(q t) k -> q t k", t=X_TILES)
        out_view = out.rearrange("(q t) n -> q t n", t=X_TILES)
        w_by_pass = W.rearrange("(g u q e) c -> g u q e c", g=PASSES, u=2, q=PARTS, e=2)
        w_by_parity = W.rearrange("(a q e) c -> e q a c", a=2 * PASSES, q=PARTS, e=2)

        def column(name):
            return small.tile([PARTS, 1], F32, name=name)

        def two_columns(name):
            return small.tile([PARTS, 2], F32, name=name)

        scalar_row = keep.tile([PARTS, 4 * SLOT], BF16)
        ones = keep.tile([PARTS, PARTS], BF16)
        p_rows = keep.tile([PARTS, PARTS], BF16)
        zero = column("zero")
        unused = column("unused")
        ident = keep.tile([PARTS, PARTS], F32)
        ident_bf = keep.tile([PARTS, PARTS], BF16)
        x_sb = [keep.tile([PARTS, 2, K_DIM], BF16, name="x_sb%d" % d) for d in range(X_TILES // 2)]
        w_first = [keep.tile([PARTS, PACK, HALF_COLS], BF16, name="w_first%d" % g) for g in range(PASSES)]
        w_second = keep.tile([PARTS, PASSES, PACK, HALF_COLS], BF16)
        x_grouped = [
            keep.tile([PARTS, PASSES, PARTS * PACK], BF16, name="x_grouped%d" % t, align_bytes=64) for t in range(X_TILES)
        ]
        x_codes = keep.tile([PARTS, PASSES, ROWS], U32, align_bytes=64)
        x_scales = keep.tile([PARTS, PASSES, ROWS], U8, align_bytes=64)
        w_grouped = [
            [keep.tile([PARTS, HALF_COLS, PACK], BF16, name="w_grouped%d%d" % (g, c), align_bytes=64) for c in range(W_HALVES)]
            for g in range(PASSES)
        ]
        w_codes = keep.tile([PARTS, PASSES, COLS], U32, align_bytes=64)
        w_scales = keep.tile([PARTS, PASSES, COLS], U8, align_bytes=64)
        linear_out = [keep.tile([PARTS, K_DIM], F32, name="linear_out%d" % t) for t in range(X_TILES)]
        periodic_out = [
            keep.tile([PARTS, TILES_PER_HALF, 2 * PARTS], F32, name="periodic_out%d" % number) for number in range(PAIRS)
        ]

        scalars = small.tile([PARTS, 4], F32)
        w_and_p = two_columns("w_and_p")
        twice_if_positive = column("twice_if_positive")
        magnitudes = two_columns("magnitudes")
        folded = two_columns("folded")
        c1 = folded[:, 0:1]
        s1 = folded[:, 1:2]
        norm1 = column("norm1")
        inv_norm1 = column("inv_norm1")
        angles = two_columns("angles")
        guess = angles[:, 0:1]
        sin_cos = two_columns("sin_cos")
        times_sin = two_columns("times_sin")
        along = column("along")
        across = column("across")
        inv_along = column("inv_along")
        signed_along = column("signed_along")
        tan = column("tan")
        tan2 = column("tan2")
        tan4 = column("tan4")
        atan_low = column("atan_low")
        atan_high = column("atan_high")
        root_low = column("root_low")
        root_high = column("root_high")
        atan_over_tan = column("atan_over_tan")
        root = column("root")
        phi = column("phi")
        amp = column("amp")
        bias_radians = small.tile([PARTS, N_TILES], F32)
        bias_turns = small.tile([PARTS, N_TILES], F32)

        spread = psum.tile([PARTS, 4, SLOT], F32, tag="bank", name="spread")
        p_t = psum.tile([PARTS, PARTS], BF16, tag="bank", name="p_t")
        in_psum = {}
        in_flow = {}

        def load_scalar(place, scalar):
            nc.scalar.dma_start(
                out=scalar_row[0:1, SLOT * place : SLOT * place + 1], in_=scalar.rearrange("(o v) -> o v", o=1)
            )

        def load_x(d):
            nc.sync.dma_start(out=x_sb[d][:], in_=x_view[:, 2 * d : 2 * d + 2, :])

        def load_w_first(g, u):
            nc.sync.dma_start(out=w_first[g][:, 2 * u : 2 * u + 2, :], in_=w_by_pass[g, u][:, :, 0:HALF_COLS])

        def load_w_second(e):
            nc.sync.dma_start(
                out=w_second[:].rearrange("q g (u e) c -> q (g u) e c", e=2)[:, :, e, :], in_=w_by_parity[e][:, :, HALF_COLS:COLS]
            )

        def x_transpose(t):
            words_t = psum.tile([PARTS, 2 * PASSES, PARTS], F32, tag="bank", name="words_t")
            words = x_sb[t // 2][:, t % 2, :].bitcast(F32)
            for a in range(2 * PASSES):
                nc.tensor.transpose(out=words_t[:, a, :], in_=words[:, PARTS * a : PARTS * a + PARTS], identity=ident[:])
            in_psum["x", t] = words_t

        def x_copy(t):
            nc.scalar.copy(
                out=x_grouped[t][:].bitcast(F32).rearrange("q g (b u) -> q g b u", u=2),
                in_=in_psum["x", t][:].rearrange("q (g u) b -> q g b u", g=PASSES, u=2),
            )

        def x_quant(g, t):
            cols = slice(PARTS * t, PARTS * t + PARTS)
            nc.vector.quantize_mx(out=x_codes[:, g, cols].bitcast(FP8X4), scales=x_scales[:, g, cols], in_=x_grouped[t][:, g, :])

        def w_regroup(g, c):
            rows = w_first[g][:] if c == 0 else w_second[:, g]
            dst = w_grouped[g][c][:].rearrange("q (n r) y -> q n y r", r=4)
            src = rows.rearrange("q y (n r) -> q n y r", r=4)
            if c == 0:
                nc.vector.tensor_copy(out=dst, in_=src)
            else:
                nc.scalar.copy(out=dst, in_=src)

        def w_quant(g, c):
            cols = slice(HALF_COLS * c, HALF_COLS * c + HALF_COLS)
            nc.vector.quantize_mx(
                out=w_codes[:, g, cols].bitcast(FP8X4),
                scales=w_scales[:, g, cols],
                in_=w_grouped[g][c][:].rearrange("q n y -> q (n y)"),
            )

        def linear(t):
            nc.gpsimd.tensor_scalar(
                out=linear_out[t][:],
                in0=x_sb[t // 2][:, t % 2, :],
                scalar1=w_and_p[:, 0:1],
                scalar2=w_and_p[:, 1:2],
                op0=ALU.mult,
                op1=ALU.add,
            )

        def store_linear(t):
            nc.sync.dma_start(out=out_view[:, t, 0:K_DIM], in_=linear_out[t][:])

        def hand_w_and_p_to_gpsimd():
            nc.vector.tensor_copy(out=w_and_p[:], in_=scalars[:, 0:2])

        def spread_scalars():
            nc.tensor.matmul(
                out=spread[:].rearrange("q l s -> q (l s)"), lhsT=ones[:], rhs=scalar_row[:], start=True, stop=True
            )

        def chain_fetch():
            nc.vector.tensor_copy(out=scalars[:], in_=spread[:, :, 0])

        def chain_sign():
            nc.vector.tensor_scalar(
                out=twice_if_positive[:], in0=scalars[:, 3:4], scalar1=0.0, scalar2=2.0, op0=ALU.is_ge, op1=ALU.mult
            )
            nc.vector.scalar_tensor_tensor(
                out=magnitudes[:], in0=scalars[:, 2:4], scalar=-1.0, in1=scalars[:, 2:4], op0=ALU.mult, op1=ALU.max
            )

        def chain_fold():
            nc.vector.scalar_tensor_tensor(
                out=folded[:], in0=scalars[:, 2:4], scalar=twice_if_positive[:], in1=scalars[:, 2:4], op0=ALU.mult, op1=ALU.subtract
            )
            nc.vector.tensor_scalar(
                out=norm1[:], in0=magnitudes[:, 0:1], scalar1=magnitudes[:, 1:2], scalar2=TINY, op0=ALU.add, op1=ALU.add
            )

        def chain_invert_norm():
            nc.vector.reciprocal(out=inv_norm1[:], in_=norm1[:])

        def chain_guess():
            nc.vector.tensor_scalar(out=guess, in0=c1, scalar1=inv_norm1[:], scalar2=0.5 * math.pi, op0=ALU.mult, op1=ALU.mult)

        def chain_cos_argument():
            nc.vector.tensor_scalar(
                out=angles[:, 1:2], in0=guess, scalar1=0.5 * math.pi, scalar2=PI_BELOW, op0=ALU.add, op1=ALU.min
            )

        def chain_sin_cos():
            nc.scalar.activation(out=sin_cos[:], in_=angles[:], func=ACT.Sin)

        def chain_times_sin():
            nc.vector.tensor_scalar(out=times_sin[:], in0=folded[:], scalar1=sin_cos[:, 0:1], scalar2=TINY, op0=ALU.mult, op1=ALU.add)

        def chain_rotate():
            nc.vector.scalar_tensor_tensor(
                out=along[:], in0=s1, scalar=sin_cos[:, 1:2], in1=times_sin[:, 0:1], op0=ALU.mult, op1=ALU.add
            )
            nc.vector.scalar_tensor_tensor(
                out=across[:], in0=c1, scalar=sin_cos[:, 1:2], in1=times_sin[:, 1:2], op0=ALU.mult, op1=ALU.subtract
            )

        def chain_invert_along():
            nc.vector.reciprocal(out=inv_along[:], in_=along[:])
            nc.vector.scalar_tensor_tensor(
                out=signed_along[:], in0=along[:], scalar=twice_if_positive[:], in1=along[:], op0=ALU.mult, op1=ALU.subtract
            )

        def chain_tan():
            nc.vector.tensor_scalar(out=tan[:], in0=across[:], scalar1=inv_along[:], scalar2=None, op0=ALU.mult)

        def chain_tan2():
            nc.vector.tensor_scalar(out=tan2[:], in0=tan[:], scalar1=tan[:], scalar2=None, op0=ALU.mult)

        def chain_series_halves():
            nc.vector.tensor_scalar(out=atan_low[:], in0=tan2[:], scalar1=-1.0 / 3.0, scalar2=1.0, op0=ALU.mult, op1=ALU.add)
            nc.vector.tensor_scalar(out=atan_high[:], in0=tan2[:], scalar1=-1.0 / 7.0, scalar2=0.2, op0=ALU.mult, op1=ALU.add)
            nc.vector.tensor_scalar(out=tan4[:], in0=tan2[:], scalar1=tan2[:], scalar2=None, op0=ALU.mult)
            nc.vector.tensor_scalar(out=root_low[:], in0=tan2[:], scalar1=0.5, scalar2=1.0, op0=ALU.mult, op1=ALU.add)
            nc.vector.tensor_scalar(out=root_high[:], in0=tan2[:], scalar1=1.0 / 16.0, scalar2=-0.125, op0=ALU.mult, op1=ALU.add)

        def chain_series():
            nc.vector.tensor_scalar(
                out=atan_over_tan[:], in0=atan_high[:], scalar1=tan4[:], scalar2=atan_low[:], op0=ALU.mult, op1=ALU.add
            )
            nc.vector.tensor_scalar(out=root[:], in0=root_high[:], scalar1=tan4[:], scalar2=root_low[:], op0=ALU.mult, op1=ALU.add)

        def chain_phi_amp():
            nc.vector.tensor_scalar(out=phi[:], in0=atan_over_tan[:], scalar1=tan[:], scalar2=guess, op0=ALU.mult, op1=ALU.add)
            nc.vector.tensor_scalar(out=amp[:], in0=root[:], scalar1=signed_along[:], scalar2=None, op0=ALU.mult)

        def p_transpose():
            nc.tensor.transpose(out=p_t[:], in_=p_rows[:], identity=ident_bf[:])

        def chain_bias():
            nc.vector.tensor_scalar(out=bias_radians[:], in0=p_t[:, 0:N_TILES], scalar1=phi[:], scalar2=None, op0=ALU.add)
            nc.vector.tensor_scalar(
                out=bias_turns[:], in0=p_t[:, 0:N_TILES], scalar1=phi[:], scalar2=TURN, op0=ALU.add, op1=ALU.mult
            )

        def multiply(bank):
            h, j = bank
            z = psum.tile([PARTS, BANK], F32, tag="bank", name="z")
            n_cols = slice(PARTS * j, PARTS * j + PARTS)
            b_cols = slice(BANK * h, BANK * h + BANK)
            for g in range(PASSES):
                nc.tensor.matmul_mx(
                    out=z[:],
                    lhsT=w_codes[:, g, n_cols].bitcast(FP8X4),
                    lhsT_scale=w_scales[:, g, n_cols],
                    rhs=x_codes[:, g, b_cols].bitcast(FP8X4),
                    rhs_scale=x_scales[:, g, b_cols],
                    start=(g == 0),
                    stop=(g == PASSES - 1),
                )
            in_psum["z", bank] = z

        def whole_turns(bank):
            turns = flow.tile([PARTS, BANK], I32, name="turns")
            nc.vector.tensor_scalar(
                out=turns[:], in0=in_psum["z", bank][:], scalar1=TURN, scalar2=bias_turns[:, bank[1] : bank[1] + 1], op0=ALU.mult, op1=ALU.add
            )
            in_flow["turns", bank] = turns

        def take_turns_off(bank):
            rest = flow.tile([PARTS, BANK], F32, name="rest")
            nc.vector.scalar_tensor_tensor(
                out=rest[:], in0=in_psum["z", bank][:], scalar=TURN, in1=in_flow["turns", bank][:], op0=ALU.mult, op1=ALU.subtract
            )
            in_flow["rest", bank] = rest

        def sine(bank):
            sines = flow.tile([PARTS, BANK], F32, name="sines")
            nc.scalar.activation(
                out=sines[:], in_=in_flow["rest", bank][:], func=ACT.Sin, scale=2.0 * math.pi, bias=bias_radians[:, bank[1] : bank[1] + 1]
            )
            in_flow["sines", bank] = sines

        def transpose_back(bank):
            sines_t = psum.tile([PARTS, TILES_PER_HALF, PARTS], F32, tag="bank", name="sines_t")
            for member in range(TILES_PER_HALF):
                nc.tensor.transpose(
                    out=sines_t[:, member, :],
                    in_=in_flow["sines", bank][:, PARTS * member : PARTS * member + PARTS],
                    identity=ident[:],
                )
            in_psum["sines", bank] = sines_t

        def copy_out(position, on_vector):
            dst = periodic_out[position // 2][:, :, PARTS * (position % 2) : PARTS * (position % 2) + PARTS]
            src = in_psum["sines", BANK_ORDER[position]][:]
            if on_vector:
                nc.vector.tensor_scalar(out=dst, in0=src, scalar1=amp[:], scalar2=None, op0=ALU.mult)
            else:
                nc.scalar.activation(out=dst, in_=src, func=ACT.Copy, scale=amp[:])

        def store_pair(number):
            h, j = BANK_ORDER[2 * number]
            nc.sync.dma_start(
                out=out_view[:, TILES_PER_HALF * h : TILES_PER_HALF * h + TILES_PER_HALF, K_DIM + PARTS * j : K_DIM + PARTS * (j + 2)],
                in_=periodic_out[number][:],
            )

        ctx.enter_context(tc.manual_schedule())

        nc.vector.memset(p_rows[:], 0.0)
        nc.vector.memset(zero[:], 0.0)
        nc.vector.memset(scalar_row[:], 0.0)
        nc.vector.memset(ones[:], 1.0)
        for place, scalar in enumerate((w, p, cosine_w, sine_w)):
            load_scalar(place, scalar)
        nc.scalar.dma_start(out=p_rows[0:N_TILES, :], in_=P.rearrange("(j q) -> j q", q=PARTS))
        nc.scalar.activation(out=unused[:], in_=zero[:], func=ACT.Sin)
        make_identity(nc, ident[:])
        nc.gpsimd.tensor_copy(out=ident_bf[:], in_=ident[:])
        load_w_first(0, 0)
        load_w_first(0, 1)
        load_x(0)
        load_w_first(1, 0)
        load_w_first(1, 1)
        load_x(1)
        load_x(2)
        load_x(3)
        load_w_second(0)
        load_w_second(1)

        spread_scalars()
        for t in range(2):
            x_transpose(t)
            x_copy(t)
        w_regroup(0, 0)
        chain_fetch()
        chain_sign()
        w_quant(0, 0)
        chain_fold()
        chain_invert_norm()
        w_regroup(1, 0)
        chain_guess()
        chain_cos_argument()
        chain_sin_cos()
        for t in range(2, X_TILES):
            x_transpose(t)
            if t == 3:
                p_transpose()
            x_copy(t)
        x_quant(0, 0)
        x_quant(1, 0)
        w_quant(1, 0)
        chain_rest = [
            chain_times_sin,
            chain_rotate,
            chain_invert_along,
            chain_tan,
            chain_tan2,
            chain_series_halves,
            chain_series,
            chain_phi_amp,
            chain_bias,
        ]
        x_quants = [(g, t) for t in range(1, X_TILES) for g in range(PASSES)]
        step_before = [0, 2, 4, 6, 7, 8, 9, 10, 11]
        for count, (g, t) in enumerate(x_quants):
            if count in step_before:
                chain_rest[step_before.index(count)]()
            if count == step_before[-1]:
                hand_w_and_p_to_gpsimd()
            x_quant(g, t)
        for t in range(X_TILES):
            linear(t)
        for t in range(X_TILES - 2):
            store_linear(t)
        w_regroup(1, 1)
        w_regroup(0, 1)
        for position in range(BANKS_AHEAD):
            multiply(BANK_ORDER[position])

        for number in range(PAIRS):
            first, second = BANK_ORDER[2 * number], BANK_ORDER[2 * number + 1]
            whole_turns(first)
            whole_turns(second)
            take_turns_off(first)
            take_turns_off(second)
            if number < PASSES:
                w_quant(PASSES - 1 - number, 1)
            sine(first)
            sine(second)
            if 1 <= number < PAIRS - 1:
                copy_out(2 * number - 2, False)
                copy_out(2 * number - 1, False)
                store_pair(number - 1)
            if number == 1:
                store_linear(X_TILES - 2)
                store_linear(X_TILES - 1)
            transpose_back(first)
            transpose_back(second)
            for position in range(2 * number + BANKS_AHEAD, min(2 * number + BANKS_AHEAD + 2, len(BANK_ORDER))):
                multiply(BANK_ORDER[position])

        copy_out(2 * PAIRS - 4, True)
        copy_out(2 * PAIRS - 3, True)
        store_pair(PAIRS - 2)
        copy_out(2 * PAIRS - 2, False)
        copy_out(2 * PAIRS - 1, True)
        store_pair(PAIRS - 1)
